import numpy as np
import ml_dtypes


def mxq(x, axis, fmt="e4m3"):
    dtype, down = {"e4m3": (ml_dtypes.float8_e4m3fn, 7), "e5m2": (ml_dtypes.float8_e5m2, 14)}[fmt]
    v = np.moveaxis(np.asarray(x, np.float32).astype(ml_dtypes.bfloat16).astype(np.float64), axis, -1)
    blocks = v.reshape(v.shape[:-1] + (-1, 32))
    amax = np.abs(blocks).max(-1, keepdims=True)
    byte = np.maximum(np.where(amax > 0, np.frexp(amax)[1] - 1 + 127, 0) - down, 1)
    scale = np.exp2(byte - 127.0)
    codes = (blocks / scale).astype(np.float32).astype(dtype).astype(np.float64)
    return np.moveaxis((codes * scale).reshape(v.shape), -1, axis)


WIDE = False


def mx_kscale(k):
    if not WIDE:
        return np.ones(k)
    levels = np.array([10, -10, 5, -5, 0])
    a = np.random.permutation(np.resize(levels, k // 512 * 4)).reshape(k // 512, 4)
    idx = np.arange(k)
    return np.exp2(a[idx // 512, idx % 128 // 32])


BF16 = ml_dtypes.bfloat16


def bf(x):
    return np.asarray(x, np.float32).astype(BF16)


def f64(x):
    return np.asarray(x).astype(np.float64)


E2M1 = np.array([0.0, 0.5, 1.0, 1.5, 2.0, 3.0, 4.0, 6.0, -0.0, -0.5, -1.0, -1.5, -2.0, -3.0, -4.0, -6.0])


def pack_weight(w, fmt):
    k, n = w.shape
    w = f64(bf(w)).reshape(k // 32, 32, n)
    amax = np.abs(w).max(1)
    if fmt == "e4m3":
        byte = np.frexp(amax)[1] - 1 + 127 - 7
    else:
        mant, ex = np.frexp(amax / 6.0)
        byte = np.where(mant > 0.5, ex, ex - 1) + 127
    byte = np.clip(np.where(amax > 0, byte, 1), 1, 254)
    scaled = (w * np.exp2(127.0 - byte)[:, None, :]).reshape(k, n).astype(np.float32)
    by_word = np.ascontiguousarray(scaled.reshape(k // 512, 128, 4, n).transpose(0, 1, 3, 2))
    if fmt == "e4m3":
        words = by_word.astype(ml_dtypes.float8_e4m3fn).view(np.uint8)
    else:
        c = by_word.astype(ml_dtypes.float4_e2m1fn).view(np.uint8) & 0xF
        words = c[..., 0::2] | (c[..., 1::2] << 4)
    return np.ascontiguousarray(words), np.ascontiguousarray(byte.astype(np.uint8).reshape(k // 512, 16, n))


def unpack_weight(words, scales, fmt):
    g, p, n, _ = words.shape
    if fmt == "e4m3":
        vals = np.ascontiguousarray(words).view(ml_dtypes.float8_e4m3fn).astype(np.float64)
    else:
        nib = np.empty((g, p, n, 4), np.uint8)
        nib[..., 0::2] = words & 0xF
        nib[..., 1::2] = words >> 4
        vals = E2M1[nib]
    vals = vals * np.repeat(np.exp2(scales.astype(np.float64) - 127.0), 8, axis=1)[..., None]
    return vals.transpose(0, 1, 3, 2).reshape(g * 512, n)


M, B, T, D, P = 2, 128, 2, 2560, 2048
LN_EPS = 1e-5
NORM_EPS = 1e-12


def erf(v):
    a = np.clip(v, -6.0, 6.0)
    term = a.copy()
    total = a.copy()
    for n in range(1, 130):
        term = term * (2.0 * a * a / (2 * n + 1))
        total = total + term
    return 2.0 / np.sqrt(np.pi) * np.exp(-a * a) * total


def gelu_erf(v):
    return 0.5 * v * (1.0 + erf(v / np.sqrt(2.0)))


def setup_inputs():
    s = mx_kscale(D)
    feats = bf(np.random.standard_normal((M, B, T, D)) * s)
    w1 = np.random.standard_normal((M, D, D)) * np.sqrt(T / D) / s[None, :, None]
    b1 = bf(np.random.standard_normal((M, D)) * 0.3)
    w2 = np.random.standard_normal((M, D, P)) * 0.6 / np.sqrt(D)
    b2 = bf(0.25 + np.random.standard_normal((M, P)) * 0.15)
    gamma = bf(1.0 + np.random.standard_normal((M, P)) * 0.2)
    beta = bf(np.random.standard_normal((M, P)) * 0.3)
    w1_words, w1_scales = pack_weight(w1.reshape(-1, D), "e4m3")
    w2_words, w2_scales = pack_weight(w2.reshape(-1, P), "e4m3")
    return {"feats": feats,
            "W1_words": w1_words,
            "W1_scales": w1_scales,
            "b1": b1,
            "W2_words": w2_words,
            "W2_scales": w2_scales,
            "b2": b2,
            "gamma": gamma,
            "beta": beta}


def reference(feats, W1_words, W1_scales, b1, W2_words, W2_scales, b2, gamma, beta):
    pooled = f64(feats).mean(axis=2)
    h = gelu_erf((mxq(pooled, 2, "e4m3") @ unpack_weight(W1_words, W1_scales, "e4m3").reshape(M, D, D)) + f64(b1)[:, None, :])
    z = (mxq(h, 2, "e4m3") @ unpack_weight(W2_words, W2_scales, "e4m3").reshape(M, D, P)) + f64(b2)[:, None, :]
    mu = z.mean(axis=-1, keepdims=True)
    var = np.mean((z - mu) ** 2, axis=-1, keepdims=True)
    z = (z - mu) / np.sqrt(var + LN_EPS) * f64(gamma)[:, None, :] + f64(beta)[:, None, :]
    n = np.sqrt(np.sum(z * z, axis=-1, keepdims=True))
    return z / np.maximum(n, NORM_EPS)

@@ -1,0 +1,258 @@
+from contextlib import ExitStack
+
+import concourse.mybir as mybir
+from concourse.masks import make_identity
+
+F32 = mybir.dt.float32
+BF16 = mybir.dt.bfloat16
+I32 = mybir.dt.int32
+U32 = mybir.dt.uint32
+U8 = mybir.dt.uint8
+FP8X4 = mybir.dt.float8_e4m3fn_x4
+ACT = mybir.ActivationFunctionType
+ALU = mybir.AluOpType
+AXIS = mybir.AxisListType
+
+P = 128
+PACK = 4
+K_PASS = P * PACK
+N_TILE = 512
+MODS = 2
+STEPS = 2
+D = 2560
+PROJ = 2048
+PASSES = D // K_PASS
+H_TILES = D // N_TILE
+Z_TILES = PROJ // N_TILE
+PLANES_PER_SLOT = 4
+LN_EPS = 1e-5
+NORM_EPS = 1e-12
+
+B1_ROW = 0
+B2_ROW = B1_ROW + MODS * H_TILES
+GAMMA_ROW = B2_ROW + MODS * Z_TILES
+BETA_ROW = GAMMA_ROW + MODS * Z_TILES
+VEC_ROWS = BETA_ROW + MODS * Z_TILES
+
+FLOPS = 2 * MODS * P * D * (D + PROJ)
+
+
+def load_scale_planes(nc, planes, scales):
+    groups = scales.shape[0]
+    for first in range(0, groups, PLANES_PER_SLOT):
+        count = min(PLANES_PER_SLOT, groups - first)
+        for quadrant in range(4):
+            nc.sync.dma_start(
+                out=planes[32 * quadrant : 32 * quadrant + 4 * count, first // PLANES_PER_SLOT, :].bitcast(I32),
+                in_=scales[first : first + count, 4 * quadrant : 4 * quadrant + 4, :].bitcast(I32),
+            )
+
+
+def weight_scale_plane(planes, g, cols):
+    return planes[4 * (g % PLANES_PER_SLOT) : P, g // PLANES_PER_SLOT, cols]
+
+
+def tile_semanticaligner_w_e_kernel(
+    tc, feats, W1_words, W1_scales, b1, W2_words, W2_scales, b2, gamma, beta, out
+):
+    nc = tc.nc
+    with ExitStack() as ctx:
+        const = ctx.enter_context(tc.tile_pool(name="const", bufs=1))
+        feats_pool = ctx.enter_context(tc.tile_pool(name="feats", bufs=1))
+        w1_pool = ctx.enter_context(tc.tile_pool(name="w1", bufs=5))
+        w2_pool = ctx.enter_context(tc.tile_pool(name="w2", bufs=6))
+        rows_pool = ctx.enter_context(tc.tile_pool(name="rows", bufs=2))
+        operand_pool = ctx.enter_context(tc.tile_pool(name="operand", bufs=2))
+        work = ctx.enter_context(tc.tile_pool(name="work", bufs=3))
+        z_pool = ctx.enter_context(tc.tile_pool(name="z", bufs=2))
+        small = ctx.enter_context(tc.tile_pool(name="small", bufs=2))
+        acc_pool = ctx.enter_context(tc.psum_pool(name="acc", bufs=5))
+        turn_pool = ctx.enter_context(tc.psum_pool(name="turn", bufs=3))
+
+        ident_f32 = const.tile([P, P], F32)
+        make_identity(nc, ident_f32[:])
+        ident_bf16 = const.tile([P, P], BF16)
+        make_identity(nc, ident_bf16[:])
+        ln_eps = const.tile([P, 1], F32)
+        nc.vector.memset(ln_eps[:], LN_EPS)
+
+        slots = -(-MODS * PASSES // PLANES_PER_SLOT)
+        w1_planes = const.tile([P, slots, D], U8, align_bytes=64)
+        nc.vector.memset(w1_planes[:].bitcast(I32), 0)
+        w2_planes = const.tile([P, slots, PROJ], U8, align_bytes=64)
+        nc.vector.memset(w2_planes[:].bitcast(I32), 0)
+
+        vec_rows = const.tile([P, N_TILE], BF16)
+        nc.vector.memset(vec_rows[:], 0.0)
+        for first_row, vec in ((B1_ROW, b1), (B2_ROW, b2), (GAMMA_ROW, gamma), (BETA_ROW, beta)):
+            pieces = vec.rearrange("m (j c) -> (m j) c", c=N_TILE)
+            nc.scalar.dma_start(out=vec_rows[first_row : first_row + pieces.shape[0], :], in_=pieces)
+
+        feats_sb = []
+        w1_sb = []
+        w2_sb = []
+
+        def load_feats(m):
+            f = feats_pool.tile([P, STEPS, D], BF16, name="feats%d" % m, tag="feats")
+            nc.sync.dma_start(out=f[:], in_=feats[m])
+            feats_sb.append(f)
+
+        def load_w1(m):
+            for g in range(m * PASSES, (m + 1) * PASSES):
+                w = w1_pool.tile([P, PACK * D], U8, name="w1_%d" % g, tag="w1", align_bytes=64)
+                nc.sync.dma_start(out=w[:].bitcast(I32), in_=W1_words[g].rearrange("p n t -> p (n t)").bitcast(I32))
+                w1_sb.append(w)
+
+        def load_w2(m):
+            for g in range(m * PASSES, (m + 1) * PASSES):
+                w = w2_pool.tile([P, PACK * PROJ], U8, name="w2_%d" % g, tag="w2", align_bytes=64)
+                words = W2_words[g].rearrange("p n t -> p (n t)")
+                pieces = Z_TILES if g == (m + 1) * PASSES - 1 else 1
+                width = PACK * PROJ // pieces
+                for c in range(pieces):
+                    part = slice(c * width, (c + 1) * width)
+                    nc.sync.dma_start(out=w[:, part].bitcast(I32), in_=words[:, part].bitcast(I32))
+                w2_sb.append(w)
+
+        load_feats(0)
+        load_scale_planes(nc, w1_planes, W1_scales)
+        load_scale_planes(nc, w2_planes, W2_scales)
+        load_w1(0)
+        load_feats(1)
+        load_w1(1)
+        load_w2(0)
+        load_w2(1)
+
+        spread = const.tile([P, VEC_ROWS, N_TILE], BF16)
+
+        def spread_rows(first_row, last_row):
+            for r in range(first_row, last_row, 2):
+                bank = turn_pool.tile([P, 2, N_TILE], BF16, name="bank", tag="turn")
+                for i in range(2):
+                    nc.tensor.matmul(
+                        out=bank[:, i, :],
+                        lhsT=ident_bf16[:, r + i : r + i + 1].to_broadcast([P, P]),
+                        rhs=vec_rows[:],
+                        start=True,
+                        stop=True,
+                    )
+                nc.scalar.copy(out=spread[:, r : r + 2, :], in_=bank[:])
+
+        def quantise_pass(rows, g, codes, planes):
+            words = rows[:].bitcast(F32)
+            turned = turn_pool.tile([P, 2, P], F32, name="turned", tag="turn")
+            for u in range(2):
+                nc.tensor.transpose(
+                    turned[:, u, :], words[:, (K_PASS // 2) * g + u : (K_PASS // 2) * (g + 1) : 2], ident_f32[:]
+                )
+            grouped = work.tile([P, P * PACK], BF16, name="grouped", tag="grouped", align_bytes=64)
+            nc.scalar.copy(
+                out=grouped[:].bitcast(F32).rearrange("p (b u) -> p b u", u=2),
+                in_=turned[:].rearrange("p u b -> p b u"),
+            )
+            nc.vector.quantize_mx(out=codes[:, g, :].bitcast(FP8X4), scales=planes[:, g, :], in_=grouped[:])
+
+        def new_operand(kind):
+            codes = operand_pool.tile([P, PASSES, P], U32, name=kind + "_codes", tag=kind + "_codes", align_bytes=64)
+            planes = operand_pool.tile([P, PASSES, P], U8, name=kind + "_planes", tag=kind + "_planes", align_bytes=64)
+            return codes, planes
+
+        def pool_over_time(m):
+            pooled = rows_pool.tile([P, D], BF16, name="pooled", tag="rows")
+            codes, planes = new_operand("x")
+            for g in range(PASSES):
+                cols = slice(g * K_PASS, (g + 1) * K_PASS)
+                total = work.tile([P, K_PASS], F32, name="total", tag="total")
+                nc.vector.tensor_add(out=total[:], in0=feats_sb[m][:, 0, cols], in1=feats_sb[m][:, 1, cols])
+                nc.vector.tensor_scalar_mul(out=pooled[:, cols], in0=total[:], scalar1=1.0 / STEPS)
+                quantise_pass(pooled, g, codes, planes)
+            return codes, planes
+
+        def linear(m, operand, w_sb, w_planes, n_tiles):
+            codes, planes = operand
+            banks = [acc_pool.tile([P, N_TILE], F32, name="acc%d" % j, tag="acc") for j in range(n_tiles)]
+            for i in range(PASSES):
+                g = m * PASSES + i
+                for j in range(n_tiles):
+                    nc.tensor.matmul_mx(
+                        out=banks[j][:],
+                        lhsT=codes[:, i, :].bitcast(FP8X4),
+                        lhsT_scale=planes[:, i, :],
+                        rhs=w_sb[g][:, PACK * N_TILE * j : PACK * N_TILE * (j + 1)].bitcast(FP8X4),
+                        rhs_scale=weight_scale_plane(w_planes, g, slice(N_TILE * j, N_TILE * (j + 1))),
+                        start=(i == 0),
+                        stop=(i == PASSES - 1),
+                    )
+            return banks
+
+        def gelu_and_quantise(m, banks):
+            h = rows_pool.tile([P, D], BF16, name="h", tag="rows")
+            codes, planes = new_operand("h")
+            for j in range(H_TILES):
+                biased = work.tile([P, N_TILE], F32, name="biased", tag="biased")
+                nc.vector.tensor_add(out=biased[:], in0=banks[j][:], in1=spread[:, B1_ROW + m * H_TILES + j, :])
+                nc.scalar.activation(out=h[:, N_TILE * j : N_TILE * (j + 1)], in_=biased[:], func=ACT.Gelu)
+                quantise_pass(h, j, codes, planes)
+            return codes, planes
+
+        def normalise_and_store(m, banks):
+            tiles = [slice(N_TILE * c, N_TILE * (c + 1)) for c in range(Z_TILES)]
+            z = z_pool.tile([P, PROJ], F32, name="z", tag="z")
+            stats = small.tile([P, Z_TILES, 6], F32, name="stats", tag="stats")
+            for c in range(Z_TILES):
+                nc.vector.tensor_add(out=z[:, tiles[c]], in0=banks[c][:], in1=spread[:, B2_ROW + m * Z_TILES + c, :])
+                nc.vector.bn_stats(out=stats[:, c, :], in_=z[:, tiles[c]])
+            mean_var = small.tile([P, 2], F32, name="mean_var", tag="mean_var")
+            nc.vector.bn_aggr(out=mean_var[:], in_=stats[:].rearrange("p c s -> p (c s)"))
+            std = small.tile([P, 1], F32, name="std", tag="std")
+            nc.scalar.activation(out=std[:], in_=mean_var[:, 1:2], func=ACT.Sqrt, bias=ln_eps[:])
+            rstd = small.tile([P, 1], F32, name="rstd", tag="rstd")
+            nc.vector.reciprocal(out=rstd[:], in_=std[:])
+
+            for c in range(Z_TILES):
+                nc.vector.scalar_tensor_tensor(
+                    out=z[:, tiles[c]],
+                    in0=z[:, tiles[c]],
+                    scalar=mean_var[:, 0:1],
+                    in1=spread[:, GAMMA_ROW + m * Z_TILES + c, :],
+                    op0=ALU.subtract,
+                    op1=ALU.mult,
+                )
+            sumsq = small.tile([P, Z_TILES], F32, name="sumsq", tag="sumsq")
+            for c in range(Z_TILES):
+                nc.vector.scalar_tensor_tensor(
+                    out=z[:, tiles[c]],
+                    in0=z[:, tiles[c]],
+                    scalar=rstd[:],
+                    in1=spread[:, BETA_ROW + m * Z_TILES + c, :],
+                    op0=ALU.mult,
+                    op1=ALU.add,
+                )
+                square = work.tile([P, N_TILE], F32, name="square", tag="square")
+                nc.scalar.activation(out=square[:], in_=z[:, tiles[c]], func=ACT.Square, accum_out=sumsq[:, c : c + 1])
+
+            norm = small.tile([P, 1], F32, name="norm", tag="norm")
+            nc.vector.reduce_sum(out=norm[:], in_=sumsq[:], axis=AXIS.X)
+            nc.vector.tensor_scalar_max(out=norm[:], in0=norm[:], scalar1=NORM_EPS * NORM_EPS)
+            nc.scalar.sqrt(out=norm[:], in_=norm[:])
+            inv_norm = small.tile([P, 1], F32, name="inv_norm", tag="inv_norm")
+            nc.vector.reciprocal(out=inv_norm[:], in_=norm[:])
+            for c in range(Z_TILES):
+                if c % 2 == 0:
+                    nc.vector.tensor_scalar_mul(out=z[:, tiles[c]], in0=z[:, tiles[c]], scalar1=inv_norm[:])
+                else:
+                    nc.scalar.activation(out=z[:, tiles[c]], in_=z[:, tiles[c]], func=ACT.Copy, scale=inv_norm[:])
+                nc.sync.dma_start(out=out[m][:, tiles[c]], in_=z[:, tiles[c]])
+
+        spread_rows(B1_ROW, B2_ROW)
+        x0 = pool_over_time(0)
+        spread_rows(B2_ROW, VEC_ROWS)
+        s0 = linear(0, x0, w1_sb, w1_planes, H_TILES)
+        x1 = pool_over_time(1)
+        h0 = gelu_and_quantise(0, s0)
+        s1 = linear(1, x1, w1_sb, w1_planes, H_TILES)
+        h1 = gelu_and_quantise(1, s1)
+        z0 = linear(0, h0, w2_sb, w2_planes, Z_TILES)
+        normalise_and_store(0, z0)
+        z1 = linear(1, h1, w2_sb, w2_planes, Z_TILES)
+        normalise_and_store(1, z1)

@@ -68,6 +68,7 @@ def tile_semanticaligner_w_e_kernel(
         small = ctx.enter_context(tc.tile_pool(name="small", bufs=2))
         acc_pool = ctx.enter_context(tc.psum_pool(name="acc", bufs=5))
         turn_pool = ctx.enter_context(tc.psum_pool(name="turn", bufs=3))
+        ctx.enter_context(tc.manual_schedule())
 
         ident_f32 = const.tile([P, P], F32)
         make_identity(nc, ident_f32[:])
@@ -76,14 +77,15 @@ def tile_semanticaligner_w_e_kernel(
         ln_eps = const.tile([P, 1], F32)
         nc.vector.memset(ln_eps[:], LN_EPS)
 
+        vec_rows = const.tile([P, N_TILE], BF16)
+        nc.vector.memset(vec_rows[:], 0.0)
+
         slots = -(-MODS * PASSES // PLANES_PER_SLOT)
         w1_planes = const.tile([P, slots, D], U8, align_bytes=64)
         nc.vector.memset(w1_planes[:].bitcast(I32), 0)
         w2_planes = const.tile([P, slots, PROJ], U8, align_bytes=64)
         nc.vector.memset(w2_planes[:].bitcast(I32), 0)
 
-        vec_rows = const.tile([P, N_TILE], BF16)
-        nc.vector.memset(vec_rows[:], 0.0)
         for first_row, vec in ((B1_ROW, b1), (B2_ROW, b2), (GAMMA_ROW, gamma), (BETA_ROW, beta)):
             pieces = vec.rearrange("m (j c) -> (m j) c", c=N_TILE)
             nc.scalar.dma_start(out=vec_rows[first_row : first_row + pieces.shape[0], :], in_=pieces)
@@ -97,31 +99,25 @@ def tile_semanticaligner_w_e_kernel(
             nc.sync.dma_start(out=f[:], in_=feats[m])
             feats_sb.append(f)
 
-        def load_w1(m):
+        def load_weight(m, pool, words, n_cols, kept, kind):
             for g in range(m * PASSES, (m + 1) * PASSES):
-                w = w1_pool.tile([P, PACK * D], U8, name="w1_%d" % g, tag="w1", align_bytes=64)
-                nc.sync.dma_start(out=w[:].bitcast(I32), in_=W1_words[g].rearrange("p n t -> p (n t)").bitcast(I32))
-                w1_sb.append(w)
-
-        def load_w2(m):
-            for g in range(m * PASSES, (m + 1) * PASSES):
-                w = w2_pool.tile([P, PACK * PROJ], U8, name="w2_%d" % g, tag="w2", align_bytes=64)
-                words = W2_words[g].rearrange("p n t -> p (n t)")
-                pieces = Z_TILES if g == (m + 1) * PASSES - 1 else 1
-                width = PACK * PROJ // pieces
+                w = pool.tile([P, PACK * n_cols], U8, name="%s_%d" % (kind, g), tag=kind, align_bytes=64)
+                flat = words[g].rearrange("p n t -> p (n t)")
+                pieces = n_cols // N_TILE if g == (m + 1) * PASSES - 1 else 1
+                width = PACK * n_cols // pieces
                 for c in range(pieces):
                     part = slice(c * width, (c + 1) * width)
-                    nc.sync.dma_start(out=w[:, part].bitcast(I32), in_=words[:, part].bitcast(I32))
-                w2_sb.append(w)
+                    nc.sync.dma_start(out=w[:, part].bitcast(I32), in_=flat[:, part].bitcast(I32))
+                kept.append(w)
 
         load_feats(0)
         load_scale_planes(nc, w1_planes, W1_scales)
         load_scale_planes(nc, w2_planes, W2_scales)
-        load_w1(0)
+        load_weight(0, w1_pool, W1_words, D, w1_sb, "w1")
         load_feats(1)
-        load_w1(1)
-        load_w2(0)
-        load_w2(1)
+        load_weight(0, w2_pool, W2_words, PROJ, w2_sb, "w2")
+        load_weight(1, w1_pool, W1_words, D, w1_sb, "w1")
+        load_weight(1, w2_pool, W2_words, PROJ, w2_sb, "w2")
 
         spread = const.tile([P, VEC_ROWS, N_TILE], BF16)
 
@@ -138,7 +134,7 @@ def tile_semanticaligner_w_e_kernel(
                     )
                 nc.scalar.copy(out=spread[:, r : r + 2, :], in_=bank[:])
 
-        def quantise_pass(rows, g, codes, planes):
+        def turn_pass(rows, g):
             words = rows[:].bitcast(F32)
             turned = turn_pool.tile([P, 2, P], F32, name="turned", tag="turn")
             for u in range(2):
@@ -150,23 +146,32 @@ def tile_semanticaligner_w_e_kernel(
                 out=grouped[:].bitcast(F32).rearrange("p (b u) -> p b u", u=2),
                 in_=turned[:].rearrange("p u b -> p b u"),
             )
-            nc.vector.quantize_mx(out=codes[:, g, :].bitcast(FP8X4), scales=planes[:, g, :], in_=grouped[:])
+            return grouped
 
-        def new_operand(kind):
+        def quantise_rows(kind, rows, fill):
             codes = operand_pool.tile([P, PASSES, P], U32, name=kind + "_codes", tag=kind + "_codes", align_bytes=64)
             planes = operand_pool.tile([P, PASSES, P], U8, name=kind + "_planes", tag=kind + "_planes", align_bytes=64)
+            grouped = []
+            for step in range(PASSES + 2):
+                if step < PASSES:
+                    fill(step)
+                if 1 <= step <= PASSES:
+                    grouped.append(turn_pass(rows, step - 1))
+                if step >= 2:
+                    g = step - 2
+                    nc.vector.quantize_mx(out=codes[:, g, :].bitcast(FP8X4), scales=planes[:, g, :], in_=grouped[g][:])
             return codes, planes
 
         def pool_over_time(m):
             pooled = rows_pool.tile([P, D], BF16, name="pooled", tag="rows")
-            codes, planes = new_operand("x")
-            for g in range(PASSES):
+
+            def mean_of_steps(g):
                 cols = slice(g * K_PASS, (g + 1) * K_PASS)
                 total = work.tile([P, K_PASS], F32, name="total", tag="total")
                 nc.vector.tensor_add(out=total[:], in0=feats_sb[m][:, 0, cols], in1=feats_sb[m][:, 1, cols])
                 nc.vector.tensor_scalar_mul(out=pooled[:, cols], in0=total[:], scalar1=1.0 / STEPS)
-                quantise_pass(pooled, g, codes, planes)
-            return codes, planes
+
+            return quantise_rows("x", pooled, mean_of_steps)
 
         def linear(m, operand, w_sb, w_planes, n_tiles):
             codes, planes = operand
@@ -187,13 +192,17 @@ def tile_semanticaligner_w_e_kernel(
 
         def gelu_and_quantise(m, banks):
             h = rows_pool.tile([P, D], BF16, name="h", tag="rows")
-            codes, planes = new_operand("h")
-            for j in range(H_TILES):
+
+            def bias_and_gelu(j):
                 biased = work.tile([P, N_TILE], F32, name="biased", tag="biased")
                 nc.vector.tensor_add(out=biased[:], in0=banks[j][:], in1=spread[:, B1_ROW + m * H_TILES + j, :])
                 nc.scalar.activation(out=h[:, N_TILE * j : N_TILE * (j + 1)], in_=biased[:], func=ACT.Gelu)
-                quantise_pass(h, j, codes, planes)
-            return codes, planes
+
+            return quantise_rows("h", h, bias_and_gelu)
+
+        def preload_table(func):
+            unused = small.tile([P, 1], F32, name="unused", tag="unused")
+            nc.scalar.activation(out=unused[:], in_=ln_eps[:], func=func)
 
         def normalise_and_store(m, banks):
             tiles = [slice(N_TILE * c, N_TILE * (c + 1)) for c in range(Z_TILES)]
@@ -247,12 +256,10 @@ def tile_semanticaligner_w_e_kernel(
         spread_rows(B1_ROW, B2_ROW)
         x0 = pool_over_time(0)
         spread_rows(B2_ROW, VEC_ROWS)
-        s0 = linear(0, x0, w1_sb, w1_planes, H_TILES)
+        h0 = gelu_and_quantise(0, linear(0, x0, w1_sb, w1_planes, H_TILES))
         x1 = pool_over_time(1)
-        h0 = gelu_and_quantise(0, s0)
-        s1 = linear(1, x1, w1_sb, w1_planes, H_TILES)
-        h1 = gelu_and_quantise(1, s1)
-        z0 = linear(0, h0, w2_sb, w2_planes, Z_TILES)
-        normalise_and_store(0, z0)
-        z1 = linear(1, h1, w2_sb, w2_planes, Z_TILES)
-        normalise_and_store(1, z1)
+        normalise_and_store(0, linear(0, h0, w2_sb, w2_planes, Z_TILES))
+        preload_table(ACT.Gelu)
+        h1 = gelu_and_quantise(1, linear(1, x1, w1_sb, w1_planes, H_TILES))
+        preload_table(ACT.Sqrt)
+        normalise_and_store(1, linear(1, h1, w2_sb, w2_planes, Z_TILES))

@@ -58,7 +58,7 @@ def tile_semanticaligner_w_e_kernel(
     nc = tc.nc
     with ExitStack() as ctx:
         const = ctx.enter_context(tc.tile_pool(name="const", bufs=1))
-        feats_pool = ctx.enter_context(tc.tile_pool(name="feats", bufs=1))
+        feats_pool = ctx.enter_context(tc.tile_pool(name="feats", bufs=2))
         w1_pool = ctx.enter_context(tc.tile_pool(name="w1", bufs=5))
         w2_pool = ctx.enter_context(tc.tile_pool(name="w2", bufs=6))
         rows_pool = ctx.enter_context(tc.tile_pool(name="rows", bufs=2))
@@ -68,7 +68,6 @@ def tile_semanticaligner_w_e_kernel(
         small = ctx.enter_context(tc.tile_pool(name="small", bufs=2))
         acc_pool = ctx.enter_context(tc.psum_pool(name="acc", bufs=5))
         turn_pool = ctx.enter_context(tc.psum_pool(name="turn", bufs=3))
-        ctx.enter_context(tc.manual_schedule())
 
         ident_f32 = const.tile([P, P], F32)
         make_identity(nc, ident_f32[:])
@@ -99,11 +98,11 @@ def tile_semanticaligner_w_e_kernel(
             nc.sync.dma_start(out=f[:], in_=feats[m])
             feats_sb.append(f)
 
-        def load_weight(m, pool, words, n_cols, kept, kind):
+        def load_weight(m, pool, words, n_cols, kept, kind, tapered=False):
             for g in range(m * PASSES, (m + 1) * PASSES):
                 w = pool.tile([P, PACK * n_cols], U8, name="%s_%d" % (kind, g), tag=kind, align_bytes=64)
                 flat = words[g].rearrange("p n t -> p (n t)")
-                pieces = n_cols // N_TILE if g == (m + 1) * PASSES - 1 else 1
+                pieces = n_cols // N_TILE if tapered and g == (m + 1) * PASSES - 1 else 1
                 width = PACK * n_cols // pieces
                 for c in range(pieces):
                     part = slice(c * width, (c + 1) * width)
@@ -111,20 +110,21 @@ def tile_semanticaligner_w_e_kernel(
                 kept.append(w)
 
         load_feats(0)
+        load_feats(1)
         load_scale_planes(nc, w1_planes, W1_scales)
         load_scale_planes(nc, w2_planes, W2_scales)
         load_weight(0, w1_pool, W1_words, D, w1_sb, "w1")
-        load_feats(1)
         load_weight(0, w2_pool, W2_words, PROJ, w2_sb, "w2")
         load_weight(1, w1_pool, W1_words, D, w1_sb, "w1")
-        load_weight(1, w2_pool, W2_words, PROJ, w2_sb, "w2")
+        load_weight(1, w2_pool, W2_words, PROJ, w2_sb, "w2", tapered=True)
 
         spread = const.tile([P, VEC_ROWS, N_TILE], BF16)
 
-        def spread_rows(first_row, last_row):
-            for r in range(first_row, last_row, 2):
+        def spread_rows(first_row, count):
+            for r in range(first_row, first_row + count, 2):
+                n = min(2, first_row + count - r)
                 bank = turn_pool.tile([P, 2, N_TILE], BF16, name="bank", tag="turn")
-                for i in range(2):
+                for i in range(n):
                     nc.tensor.matmul(
                         out=bank[:, i, :],
                         lhsT=ident_bf16[:, r + i : r + i + 1].to_broadcast([P, P]),
@@ -132,7 +132,10 @@ def tile_semanticaligner_w_e_kernel(
                         start=True,
                         stop=True,
                     )
-                nc.scalar.copy(out=spread[:, r : r + 2, :], in_=bank[:])
+                if (r // 2) % 2 == 0:
+                    nc.scalar.copy(out=spread[:, r : r + n, :], in_=bank[:, 0:n, :])
+                else:
+                    nc.vector.tensor_copy(out=spread[:, r : r + n, :], in_=bank[:, 0:n, :])
 
         def turn_pass(rows, g):
             words = rows[:].bitcast(F32)
@@ -148,18 +151,20 @@ def tile_semanticaligner_w_e_kernel(
             )
             return grouped
 
-        def quantise_rows(kind, rows, fill):
+        def quantise_rows(kind, rows, fill, use):
             codes = operand_pool.tile([P, PASSES, P], U32, name=kind + "_codes", tag=kind + "_codes", align_bytes=64)
             planes = operand_pool.tile([P, PASSES, P], U8, name=kind + "_planes", tag=kind + "_planes", align_bytes=64)
             grouped = []
-            for step in range(PASSES + 2):
+            for step in range(PASSES + 3):
                 if step < PASSES:
                     fill(step)
                 if 1 <= step <= PASSES:
                     grouped.append(turn_pass(rows, step - 1))
-                if step >= 2:
+                if 2 <= step <= PASSES + 1:
                     g = step - 2
                     nc.vector.quantize_mx(out=codes[:, g, :].bitcast(FP8X4), scales=planes[:, g, :], in_=grouped[g][:])
+                if step >= 3:
+                    use(step - 3, codes, planes)
             return codes, planes
 
         def pool_over_time(m):
@@ -167,44 +172,50 @@ def tile_semanticaligner_w_e_kernel(
 
             def mean_of_steps(g):
                 cols = slice(g * K_PASS, (g + 1) * K_PASS)
-                total = work.tile([P, K_PASS], F32, name="total", tag="total")
+                total = work.tile([P, K_PASS], BF16, name="total", tag="total")
                 nc.vector.tensor_add(out=total[:], in0=feats_sb[m][:, 0, cols], in1=feats_sb[m][:, 1, cols])
                 nc.vector.tensor_scalar_mul(out=pooled[:, cols], in0=total[:], scalar1=1.0 / STEPS)
 
-            return quantise_rows("x", pooled, mean_of_steps)
+            return quantise_rows("x", pooled, mean_of_steps, lambda g, codes, planes: None)
 
-        def linear(m, operand, w_sb, w_planes, n_tiles):
-            codes, planes = operand
-            banks = [acc_pool.tile([P, N_TILE], F32, name="acc%d" % j, tag="acc") for j in range(n_tiles)]
-            for i in range(PASSES):
-                g = m * PASSES + i
-                for j in range(n_tiles):
-                    nc.tensor.matmul_mx(
-                        out=banks[j][:],
-                        lhsT=codes[:, i, :].bitcast(FP8X4),
-                        lhsT_scale=planes[:, i, :],
-                        rhs=w_sb[g][:, PACK * N_TILE * j : PACK * N_TILE * (j + 1)].bitcast(FP8X4),
-                        rhs_scale=weight_scale_plane(w_planes, g, slice(N_TILE * j, N_TILE * (j + 1))),
-                        start=(i == 0),
-                        stop=(i == PASSES - 1),
-                    )
-            return banks
+        def open_banks(n_tiles):
+            return [acc_pool.tile([P, N_TILE], F32, name="acc%d" % j, tag="acc") for j in range(n_tiles)]
 
-        def gelu_and_quantise(m, banks):
+        def mx_pass(m, i, codes, planes, w_sb, w_planes, banks):
+            g = m * PASSES + i
+            for j in range(len(banks)):
+                nc.tensor.matmul_mx(
+                    out=banks[j][:],
+                    lhsT=codes[:, i, :].bitcast(FP8X4),
+                    lhsT_scale=planes[:, i, :],
+                    rhs=w_sb[g][:, PACK * N_TILE * j : PACK * N_TILE * (j + 1)].bitcast(FP8X4),
+                    rhs_scale=weight_scale_plane(w_planes, g, slice(N_TILE * j, N_TILE * (j + 1))),
+                    start=(i == 0),
+                    stop=(i == PASSES - 1),
+                )
+
+        def gelu_and_project(m, s_banks):
             h = rows_pool.tile([P, D], BF16, name="h", tag="rows")
+            z_banks = []
 
             def bias_and_gelu(j):
                 biased = work.tile([P, N_TILE], F32, name="biased", tag="biased")
-                nc.vector.tensor_add(out=biased[:], in0=banks[j][:], in1=spread[:, B1_ROW + m * H_TILES + j, :])
+                nc.vector.tensor_add(out=biased[:], in0=s_banks[j][:], in1=spread[:, B1_ROW + m * H_TILES + j, :])
                 nc.scalar.activation(out=h[:, N_TILE * j : N_TILE * (j + 1)], in_=biased[:], func=ACT.Gelu)
 
-            return quantise_rows("h", h, bias_and_gelu)
+            def project(i, codes, planes):
+                if i == 0:
+                    z_banks.extend(open_banks(Z_TILES))
+                mx_pass(m, i, codes, planes, w2_sb, w2_planes, z_banks)
+
+            quantise_rows("h", h, bias_and_gelu, project)
+            return z_banks
 
         def preload_table(func):
             unused = small.tile([P, 1], F32, name="unused", tag="unused")
             nc.scalar.activation(out=unused[:], in_=ln_eps[:], func=func)
 
-        def normalise_and_store(m, banks):
+        def normalise_and_store(m, banks, next_func):
             tiles = [slice(N_TILE * c, N_TILE * (c + 1)) for c in range(Z_TILES)]
             z = z_pool.tile([P, PROJ], F32, name="z", tag="z")
             stats = small.tile([P, Z_TILES, 6], F32, name="stats", tag="stats")
@@ -218,15 +229,15 @@ def tile_semanticaligner_w_e_kernel(
             rstd = small.tile([P, 1], F32, name="rstd", tag="rstd")
             nc.vector.reciprocal(out=rstd[:], in_=std[:])
 
-            for c in range(Z_TILES):
-                nc.vector.scalar_tensor_tensor(
-                    out=z[:, tiles[c]],
-                    in0=z[:, tiles[c]],
-                    scalar=mean_var[:, 0:1],
-                    in1=spread[:, GAMMA_ROW + m * Z_TILES + c, :],
-                    op0=ALU.subtract,
-                    op1=ALU.mult,
-                )
+            first_gamma = GAMMA_ROW + m * Z_TILES
+            nc.vector.scalar_tensor_tensor(
+                out=z[:],
+                in0=z[:],
+                scalar=mean_var[:, 0:1],
+                in1=spread[:, first_gamma : first_gamma + Z_TILES, :].rearrange("p r c -> p (r c)"),
+                op0=ALU.subtract,
+                op1=ALU.mult,
+            )
             sumsq = small.tile([P, Z_TILES], F32, name="sumsq", tag="sumsq")
             for c in range(Z_TILES):
                 nc.vector.scalar_tensor_tensor(
@@ -244,6 +255,8 @@ def tile_semanticaligner_w_e_kernel(
             nc.vector.reduce_sum(out=norm[:], in_=sumsq[:], axis=AXIS.X)
             nc.vector.tensor_scalar_max(out=norm[:], in0=norm[:], scalar1=NORM_EPS * NORM_EPS)
             nc.scalar.sqrt(out=norm[:], in_=norm[:])
+            if next_func is not None:
+                preload_table(next_func)
             inv_norm = small.tile([P, 1], F32, name="inv_norm", tag="inv_norm")
             nc.vector.reciprocal(out=inv_norm[:], in_=norm[:])
             for c in range(Z_TILES):
@@ -253,13 +266,24 @@ def tile_semanticaligner_w_e_kernel(
                     nc.scalar.activation(out=z[:, tiles[c]], in_=z[:, tiles[c]], func=ACT.Copy, scale=inv_norm[:])
                 nc.sync.dma_start(out=out[m][:, tiles[c]], in_=z[:, tiles[c]])
 
-        spread_rows(B1_ROW, B2_ROW)
+        def first_linear(m, operand, after_pass):
+            banks = open_banks(H_TILES)
+            for i in range(PASSES):
+                mx_pass(m, i, operand[0], operand[1], w1_sb, w1_planes, banks)
+                after_pass(i)
+            return banks
+
+        def spread_gamma_beta(i):
+            if i < (VEC_ROWS - GAMMA_ROW) // Z_TILES:
+                spread_rows(GAMMA_ROW + Z_TILES * i, Z_TILES)
+
+        spread_rows(B1_ROW, MODS * H_TILES)
         x0 = pool_over_time(0)
-        spread_rows(B2_ROW, VEC_ROWS)
-        h0 = gelu_and_quantise(0, linear(0, x0, w1_sb, w1_planes, H_TILES))
         x1 = pool_over_time(1)
-        normalise_and_store(0, linear(0, h0, w2_sb, w2_planes, Z_TILES))
-        preload_table(ACT.Gelu)
-        h1 = gelu_and_quantise(1, linear(1, x1, w1_sb, w1_planes, H_TILES))
+        spread_rows(B2_ROW, MODS * Z_TILES)
+        z0 = gelu_and_project(0, first_linear(0, x0, spread_gamma_beta))
         preload_table(ACT.Sqrt)
-        normalise_and_store(1, linear(1, h1, w2_sb, w2_planes, Z_TILES))
+        normalise_and_store(0, z0, ACT.Gelu)
+        z1 = gelu_and_project(1, first_linear(1, x1, lambda i: None))
+        preload_table(ACT.Sqrt)
+        normalise_and_store(1, z1, None)

@@ -25,27 +25,30 @@ PASSES = D // K_PASS
 H_TILES = D // N_TILE
 Z_TILES = PROJ // N_TILE
 PLANES_PER_SLOT = 4
+W1_CHUNKS = ((2560,), (1536, 1024))
+W2_CHUNKS = ((2048,), (1024, 512, 512))
 LN_EPS = 1e-5
 NORM_EPS = 1e-12
 
-B1_ROW = 0
-B2_ROW = B1_ROW + MODS * H_TILES
-GAMMA_ROW = B2_ROW + MODS * Z_TILES
-BETA_ROW = GAMMA_ROW + MODS * Z_TILES
-VEC_ROWS = BETA_ROW + MODS * Z_TILES
+EARLY_COLS = W2_CHUNKS[1][0]
+VEC_ROW = 2 * P
+B1_AT = 0
+B2_AT = B1_AT + MODS * D
+GAMMA_AT = B2_AT + MODS * PROJ
+BETA_AT = GAMMA_AT + MODS * PROJ
+VEC_LEN = BETA_AT + MODS * PROJ
 
 FLOPS = 2 * MODS * P * D * (D + PROJ)
 
 
-def load_scale_planes(nc, planes, scales):
-    groups = scales.shape[0]
-    for first in range(0, groups, PLANES_PER_SLOT):
-        count = min(PLANES_PER_SLOT, groups - first)
-        for quadrant in range(4):
-            nc.sync.dma_start(
-                out=planes[32 * quadrant : 32 * quadrant + 4 * count, first // PLANES_PER_SLOT, :].bitcast(I32),
-                in_=scales[first : first + count, 4 * quadrant : 4 * quadrant + 4, :].bitcast(I32),
-            )
+def load_scale_planes(nc, planes, scales, slot):
+    first = slot * PLANES_PER_SLOT
+    count = min(PLANES_PER_SLOT, scales.shape[0] - first)
+    for quadrant in range(4):
+        nc.gpsimd.dma_start(
+            out=planes[32 * quadrant : 32 * quadrant + 4 * count, slot, :].bitcast(F32),
+            in_=scales[first : first + count, 4 * quadrant : 4 * quadrant + 4, :].bitcast(F32),
+        )
 
 
 def weight_scale_plane(planes, g, cols):
@@ -58,84 +61,136 @@ def tile_semanticaligner_w_e_kernel(
     nc = tc.nc
     with ExitStack() as ctx:
         const = ctx.enter_context(tc.tile_pool(name="const", bufs=1))
-        feats_pool = ctx.enter_context(tc.tile_pool(name="feats", bufs=2))
-        w1_pool = ctx.enter_context(tc.tile_pool(name="w1", bufs=5))
+        w1_pool = ctx.enter_context(tc.tile_pool(name="w1", bufs=6))
         w2_pool = ctx.enter_context(tc.tile_pool(name="w2", bufs=6))
         rows_pool = ctx.enter_context(tc.tile_pool(name="rows", bufs=2))
         operand_pool = ctx.enter_context(tc.tile_pool(name="operand", bufs=2))
         work = ctx.enter_context(tc.tile_pool(name="work", bufs=3))
+        scrap = ctx.enter_context(tc.tile_pool(name="scrap", bufs=2))
         z_pool = ctx.enter_context(tc.tile_pool(name="z", bufs=2))
         small = ctx.enter_context(tc.tile_pool(name="small", bufs=2))
         acc_pool = ctx.enter_context(tc.psum_pool(name="acc", bufs=5))
         turn_pool = ctx.enter_context(tc.psum_pool(name="turn", bufs=3))
 
+        ctx.enter_context(tc.manual_schedule())
+
         ident_f32 = const.tile([P, P], F32)
         make_identity(nc, ident_f32[:])
-        ident_bf16 = const.tile([P, P], BF16)
-        make_identity(nc, ident_bf16[:])
-        ln_eps = const.tile([P, 1], F32)
-        nc.vector.memset(ln_eps[:], LN_EPS)
 
-        vec_rows = const.tile([P, N_TILE], BF16)
+        vec_rows = const.tile([P, VEC_ROW], BF16)
         nc.vector.memset(vec_rows[:], 0.0)
 
         slots = -(-MODS * PASSES // PLANES_PER_SLOT)
         w1_planes = const.tile([P, slots, D], U8, align_bytes=64)
         nc.vector.memset(w1_planes[:].bitcast(I32), 0)
+
+        pair_rows = const.tile([P, 2, VEC_ROW], BF16)
+        nc.vector.memset(pair_rows[:], 0.0)
+
+        scale_shift = const.tile([P, PROJ], BF16)
+        nc.vector.memset(scale_shift[:], 0.0)
+
         w2_planes = const.tile([P, slots, PROJ], U8, align_bytes=64)
         nc.vector.memset(w2_planes[:].bitcast(I32), 0)
 
-        for first_row, vec in ((B1_ROW, b1), (B2_ROW, b2), (GAMMA_ROW, gamma), (BETA_ROW, beta)):
-            pieces = vec.rearrange("m (j c) -> (m j) c", c=N_TILE)
-            nc.scalar.dma_start(out=vec_rows[first_row : first_row + pieces.shape[0], :], in_=pieces)
+        ln_eps = const.tile([P, 1], F32)
+        nc.vector.memset(ln_eps[:], LN_EPS)
+        minus_half = const.tile([P, 1], F32)
+        nc.vector.memset(minus_half[:], -0.5)
+        ones = const.tile([P, P], F32)
+        nc.vector.memset(ones[:], 1.0)
+        factors = const.tile([P, P], BF16)
+        nc.vector.memset(factors[:], 0.0)
 
         feats_sb = []
         w1_sb = []
         w2_sb = []
 
         def load_feats(m):
-            f = feats_pool.tile([P, STEPS, D], BF16, name="feats%d" % m, tag="feats")
+            f = w1_pool.tile([P, STEPS, D], BF16, name="feats%d" % m, tag="w1", align_bytes=64)
             nc.sync.dma_start(out=f[:], in_=feats[m])
             feats_sb.append(f)
 
-        def load_weight(m, pool, words, n_cols, kept, kind, tapered=False):
-            for g in range(m * PASSES, (m + 1) * PASSES):
-                w = pool.tile([P, PACK * n_cols], U8, name="%s_%d" % (kind, g), tag=kind, align_bytes=64)
-                flat = words[g].rearrange("p n t -> p (n t)")
-                pieces = n_cols // N_TILE if tapered and g == (m + 1) * PASSES - 1 else 1
-                width = PACK * n_cols // pieces
-                for c in range(pieces):
-                    part = slice(c * width, (c + 1) * width)
-                    nc.sync.dma_start(out=w[:, part].bitcast(I32), in_=flat[:, part].bitcast(I32))
-                kept.append(w)
+        def load_weight(m, pool, words, n_cols, chunks, kept, kind):
+            passes = range(m * PASSES, (m + 1) * PASSES)
+            start = 0
+            for width in chunks:
+                part = slice(PACK * start, PACK * (start + width))
+                for g in passes:
+                    if start == 0:
+                        kept.append(
+                            pool.tile([P, PACK * n_cols], U8, name="%s_%d" % (kind, g), tag=kind, align_bytes=64)
+                        )
+                    flat = words[g].rearrange("p n t -> p (n t)")
+                    nc.sync.dma_start(out=kept[g][:, part].bitcast(I32), in_=flat[:, part].bitcast(I32))
+                start += width
 
+        def load_vector_rows():
+            for start, vec in ((B1_AT, b1), (B2_AT, b2), (GAMMA_AT, gamma), (BETA_AT, beta)):
+                pieces = vec.rearrange("m (j c) -> (m j) c", c=VEC_ROW)
+                first_row = start // VEC_ROW
+                nc.sync.dma_start(out=vec_rows[first_row : first_row + pieces.shape[0], :], in_=pieces)
+
+        def load_last_vectors():
+            last = MODS - 1
+            for row, vec in enumerate((gamma, beta, gamma, beta)):
+                nc.sync.dma_start(out=scale_shift[row : row + 1, :], in_=vec[last : last + 1, :])
+            for at, vec in enumerate((gamma, beta)):
+                pieces = vec[last, 0:EARLY_COLS].rearrange("(j c) -> j c", c=VEC_ROW)
+                nc.sync.dma_start(out=pair_rows[0 : pieces.shape[0], at, :], in_=pieces)
+
+        load_vector_rows()
         load_feats(0)
         load_feats(1)
-        load_scale_planes(nc, w1_planes, W1_scales)
-        load_scale_planes(nc, w2_planes, W2_scales)
-        load_weight(0, w1_pool, W1_words, D, w1_sb, "w1")
-        load_weight(0, w2_pool, W2_words, PROJ, w2_sb, "w2")
-        load_weight(1, w1_pool, W1_words, D, w1_sb, "w1")
-        load_weight(1, w2_pool, W2_words, PROJ, w2_sb, "w2", tapered=True)
+        load_last_vectors()
+        for planes, scales, slot in (
+            (w1_planes, W1_scales, 0),
+            (w1_planes, W1_scales, 1),
+            (w2_planes, W2_scales, 0),
+            (w2_planes, W2_scales, 1),
+            (w1_planes, W1_scales, 2),
+            (w2_planes, W2_scales, 2),
+        ):
+            load_scale_planes(nc, planes, scales, slot)
+        ident_bf16 = const.tile([P, P], BF16)
+        make_identity(nc, ident_bf16[:])
+        for m in range(MODS):
+            load_weight(m, w1_pool, W1_words, D, W1_CHUNKS[m], w1_sb, "w1")
+            load_weight(m, w2_pool, W2_words, PROJ, W2_CHUNKS[m], w2_sb, "w2")
 
-        spread = const.tile([P, VEC_ROWS, N_TILE], BF16)
+        vec_words = const.tile([P, P], F32)
 
-        def spread_rows(first_row, count):
-            for r in range(first_row, first_row + count, 2):
-                n = min(2, first_row + count - r)
-                bank = turn_pool.tile([P, 2, N_TILE], BF16, name="bank", tag="turn")
-                for i in range(n):
-                    nc.tensor.matmul(
-                        out=bank[:, i, :],
-                        lhsT=ident_bf16[:, r + i : r + i + 1].to_broadcast([P, P]),
-                        rhs=vec_rows[:],
-                        start=True,
-                        stop=True,
-                    )
-                if (r // 2) % 2 == 0:
-                    nc.scalar.copy(out=spread[:, r : r + n, :], in_=bank[:, 0:n, :])
-                else:
-                    nc.vector.tensor_copy(out=spread[:, r : r + n, :], in_=bank[:, 0:n, :])
+        def turn_vectors():
+            words_psum = turn_pool.tile([P, P], F32, name="words_psum", tag="turn")
+            nc.tensor.transpose(words_psum[:], vec_rows[:].bitcast(F32), ident_f32[:])
+            nc.vector.tensor_copy(out=vec_words[:], in_=words_psum[:])
+
+        spread = const.tile([P, VEC_LEN], BF16)
+        spread_words = spread[:].bitcast(F32)
+        rows_per_bank = N_TILE // P
+
+        def spread_bank(first, on_scalar):
+            bank = turn_pool.tile([P, rows_per_bank, P], F32, name="bank", tag="turn")
+            for i in range(rows_per_bank):
+                nc.tensor.transpose(
+                    bank[:, i, :], vec_words[:, first + i : first + i + 1].to_broadcast([P, P]), ident_f32[:]
+                )
+            dst = spread_words[:, first * P : (first + rows_per_bank) * P]
+            src = bank[:].rearrange("p r w -> p (r w)")
+            if on_scalar:
+                nc.scalar.copy(out=dst, in_=src)
+            else:
+                nc.vector.tensor_copy(out=dst, in_=src)
+
+        def spread_banks(start, length, share):
+            firsts = range(start // VEC_ROW, (start + length) // VEC_ROW, rows_per_bank)
+            return [
+                (lambda first=first, on_scalar=(i % 2 == 0 or not share): spread_bank(first, on_scalar))
+                for i, first in enumerate(firsts)
+            ]
+
+        def spread_vec(start, m, width, cols):
+            return spread[:, start + m * width + cols.start : start + m * width + cols.stop]
 
         def turn_pass(rows, g):
             words = rows[:].bitcast(F32)
@@ -151,24 +206,25 @@ def tile_semanticaligner_w_e_kernel(
             )
             return grouped
 
-        def quantise_rows(kind, rows, fill, use):
-            codes = operand_pool.tile([P, PASSES, P], U32, name=kind + "_codes", tag=kind + "_codes", align_bytes=64)
-            planes = operand_pool.tile([P, PASSES, P], U8, name=kind + "_planes", tag=kind + "_planes", align_bytes=64)
+        def make_operand(rows, codes, planes, tiles, fill, after_step=lambda: None):
             grouped = []
-            for step in range(PASSES + 3):
-                if step < PASSES:
-                    fill(step)
-                if 1 <= step <= PASSES:
-                    grouped.append(turn_pass(rows, step - 1))
-                if 2 <= step <= PASSES + 1:
-                    g = step - 2
-                    nc.vector.quantize_mx(out=codes[:, g, :].bitcast(FP8X4), scales=planes[:, g, :], in_=grouped[g][:])
-                if step >= 3:
-                    use(step - 3, codes, planes)
-            return codes, planes
+            for step in range(len(tiles) + 2 if tiles else 0):
+                if step < len(tiles):
+                    fill(*tiles[step])
+                if 1 <= step <= len(tiles):
+                    grouped.append(turn_pass(rows, tiles[step - 1][0]))
+                if step >= 2:
+                    g = tiles[step - 2][0]
+                    nc.vector.quantize_mx(
+                        out=codes[:, g, :].bitcast(FP8X4), scales=planes[:, g, :], in_=grouped[step - 2][:]
+                    )
+                after_step()
 
-        def pool_over_time(m):
+        def pool_over_time(m, after_step):
             pooled = rows_pool.tile([P, D], BF16, name="pooled", tag="rows")
+
+            codes = operand_pool.tile([P, PASSES, P], U32, name="x_codes", tag="x_codes", align_bytes=64)
+            planes = operand_pool.tile([P, PASSES, P], U8, name="x_planes", tag="x_planes", align_bytes=64)
 
             def mean_of_steps(g):
                 cols = slice(g * K_PASS, (g + 1) * K_PASS)
@@ -176,16 +232,17 @@ def tile_semanticaligner_w_e_kernel(
                 nc.vector.tensor_add(out=total[:], in0=feats_sb[m][:, 0, cols], in1=feats_sb[m][:, 1, cols])
                 nc.vector.tensor_scalar_mul(out=pooled[:, cols], in0=total[:], scalar1=1.0 / STEPS)
 
-            return quantise_rows("x", pooled, mean_of_steps, lambda g, codes, planes: None)
+            make_operand(pooled, codes, planes, [(g,) for g in range(PASSES)], mean_of_steps, after_step)
+            return codes, planes
 
         def open_banks(n_tiles):
             return [acc_pool.tile([P, N_TILE], F32, name="acc%d" % j, tag="acc") for j in range(n_tiles)]
 
-        def mx_pass(m, i, codes, planes, w_sb, w_planes, banks):
+        def mx_pass(m, i, codes, planes, w_sb, w_planes, first_tile, banks):
             g = m * PASSES + i
-            for j in range(len(banks)):
+            for j, bank in enumerate(banks, first_tile):
                 nc.tensor.matmul_mx(
-                    out=banks[j][:],
+                    out=bank[:],
                     lhsT=codes[:, i, :].bitcast(FP8X4),
                     lhsT_scale=planes[:, i, :],
                     rhs=w_sb[g][:, PACK * N_TILE * j : PACK * N_TILE * (j + 1)].bitcast(FP8X4),
@@ -194,71 +251,101 @@ def tile_semanticaligner_w_e_kernel(
                     stop=(i == PASSES - 1),
                 )
 
-        def gelu_and_project(m, s_banks):
-            h = rows_pool.tile([P, D], BF16, name="h", tag="rows")
-            z_banks = []
-
-            def bias_and_gelu(j):
-                biased = work.tile([P, N_TILE], F32, name="biased", tag="biased")
-                nc.vector.tensor_add(out=biased[:], in0=s_banks[j][:], in1=spread[:, B1_ROW + m * H_TILES + j, :])
-                nc.scalar.activation(out=h[:, N_TILE * j : N_TILE * (j + 1)], in_=biased[:], func=ACT.Gelu)
-
-            def project(i, codes, planes):
-                if i == 0:
-                    z_banks.extend(open_banks(Z_TILES))
-                mx_pass(m, i, codes, planes, w2_sb, w2_planes, z_banks)
-
-            quantise_rows("h", h, bias_and_gelu, project)
-            return z_banks
-
         def preload_table(func):
             unused = small.tile([P, 1], F32, name="unused", tag="unused")
             nc.scalar.activation(out=unused[:], in_=ln_eps[:], func=func)
 
-        def normalise_and_store(m, banks, next_func):
+        def inverse_root(src, name):
+            root = small.tile([P, 1], F32, name=name, tag=name)
+            nc.gpsimd.tensor_tensor(out=root[:], in0=src, in1=minus_half[:], op=ALU.pow)
+            return root
+
+        def sum_of_squares(src, accum):
+            squares = scrap.tile([P, N_TILE], BF16, name="squares", tag="scalar")
+            nc.scalar.activation(out=squares[:], in_=src, func=ACT.Square, accum_out=accum)
+
+        def new_parts(name):
+            parts = small.tile([P, 2, Z_TILES], F32, name=name + "_parts", tag="parts")
+            shift = small.tile([P, 1], F32, name=name + "_shift", tag="shift")
+            return parts, shift
+
+        def shifted(m, c, bank, d, parts, shift):
+            b2_tile = spread_vec(B2_AT, m, PROJ, slice(N_TILE * c, N_TILE * (c + 1)))
+            if c == 0:
+                z = work.tile([P, N_TILE], F32, name="z0", tag="biased")
+                total = small.tile([P, 1], F32, name="total0", tag="total0")
+                nc.vector.scalar_tensor_tensor(
+                    out=z[:], in0=bank[:], scalar=1.0, in1=b2_tile, op0=ALU.mult, op1=ALU.add, accum_out=total[:]
+                )
+                nc.vector.tensor_scalar_mul(out=shift[:], in0=total[:], scalar1=1.0 / N_TILE)
+                nc.vector.tensor_scalar(
+                    out=d, in0=z[:], scalar1=shift[:], scalar2=None, op0=ALU.subtract, op1=ALU.add,
+                    accum_out=parts[:, 1, c : c + 1],
+                )
+            else:
+                nc.vector.scalar_tensor_tensor(
+                    out=d, in0=bank[:], scalar=shift[:], in1=b2_tile, op0=ALU.subtract, op1=ALU.add,
+                    accum_out=parts[:, 1, c : c + 1],
+                )
+            sum_of_squares(d, parts[:, 0, c : c + 1])
+
+        def moments(parts):
+            stats = small.tile([P, 3], F32, name="stats", tag="stats")
+            both = small.tile([P, 2], F32, name="both", tag="both")
+            nc.vector.reduce_sum(out=both[:], in_=parts[:], axis=AXIS.X)
+            nc.vector.tensor_scalar_mul(out=stats[:, 0:2], in0=both[:], scalar1=-1.0 / PROJ)
+            neg_var = small.tile([P, 1], F32, name="neg_var", tag="neg_var")
+            nc.vector.scalar_tensor_tensor(
+                out=neg_var[:], in0=stats[:, 1:2], scalar=stats[:, 1:2], in1=stats[:, 0:1], op0=ALU.mult, op1=ALU.add
+            )
+            return stats, neg_var
+
+        def normalise(m, banks):
             tiles = [slice(N_TILE * c, N_TILE * (c + 1)) for c in range(Z_TILES)]
             z = z_pool.tile([P, PROJ], F32, name="z", tag="z")
-            stats = small.tile([P, Z_TILES, 6], F32, name="stats", tag="stats")
+            parts, shift = new_parts("first")
             for c in range(Z_TILES):
-                nc.vector.tensor_add(out=z[:, tiles[c]], in0=banks[c][:], in1=spread[:, B2_ROW + m * Z_TILES + c, :])
-                nc.vector.bn_stats(out=stats[:, c, :], in_=z[:, tiles[c]])
-            mean_var = small.tile([P, 2], F32, name="mean_var", tag="mean_var")
-            nc.vector.bn_aggr(out=mean_var[:], in_=stats[:].rearrange("p c s -> p (c s)"))
-            std = small.tile([P, 1], F32, name="std", tag="std")
-            nc.scalar.activation(out=std[:], in_=mean_var[:, 1:2], func=ACT.Sqrt, bias=ln_eps[:])
-            rstd = small.tile([P, 1], F32, name="rstd", tag="rstd")
-            nc.vector.reciprocal(out=rstd[:], in_=std[:])
+                shifted(m, c, banks[c], z[:, tiles[c]], parts, shift)
+            stats, neg_var = moments(parts)
+            var_eps = small.tile([P, 1], F32, name="var_eps", tag="var_eps")
+            nc.vector.tensor_scalar(
+                out=var_eps[:], in0=neg_var[:], scalar1=-1.0, scalar2=LN_EPS, op0=ALU.mult, op1=ALU.add
+            )
+            rstd = inverse_root(var_eps[:], "rstd")
 
-            first_gamma = GAMMA_ROW + m * Z_TILES
             nc.vector.scalar_tensor_tensor(
                 out=z[:],
                 in0=z[:],
-                scalar=mean_var[:, 0:1],
-                in1=spread[:, first_gamma : first_gamma + Z_TILES, :].rearrange("p r c -> p (r c)"),
-                op0=ALU.subtract,
+                scalar=stats[:, 1:2],
+                in1=spread_vec(GAMMA_AT, m, PROJ, slice(0, PROJ)),
+                op0=ALU.add,
                 op1=ALU.mult,
             )
+            return z, rstd
+
+        def add_beta(m, z, rstd):
+            tiles = [slice(N_TILE * c, N_TILE * (c + 1)) for c in range(Z_TILES)]
             sumsq = small.tile([P, Z_TILES], F32, name="sumsq", tag="sumsq")
             for c in range(Z_TILES):
                 nc.vector.scalar_tensor_tensor(
                     out=z[:, tiles[c]],
                     in0=z[:, tiles[c]],
                     scalar=rstd[:],
-                    in1=spread[:, BETA_ROW + m * Z_TILES + c, :],
+                    in1=spread_vec(BETA_AT, m, PROJ, tiles[c]),
                     op0=ALU.mult,
                     op1=ALU.add,
                 )
-                square = work.tile([P, N_TILE], F32, name="square", tag="square")
+                square = scrap.tile([P, N_TILE], BF16, name="square", tag="scalar")
                 nc.scalar.activation(out=square[:], in_=z[:, tiles[c]], func=ACT.Square, accum_out=sumsq[:, c : c + 1])
 
+            return z, sumsq
+
+        def scale_and_store(m, z, sumsq):
+            tiles = [slice(N_TILE * c, N_TILE * (c + 1)) for c in range(Z_TILES)]
             norm = small.tile([P, 1], F32, name="norm", tag="norm")
             nc.vector.reduce_sum(out=norm[:], in_=sumsq[:], axis=AXIS.X)
             nc.vector.tensor_scalar_max(out=norm[:], in0=norm[:], scalar1=NORM_EPS * NORM_EPS)
-            nc.scalar.sqrt(out=norm[:], in_=norm[:])
-            if next_func is not None:
-                preload_table(next_func)
-            inv_norm = small.tile([P, 1], F32, name="inv_norm", tag="inv_norm")
-            nc.vector.reciprocal(out=inv_norm[:], in_=norm[:])
+            inv_norm = inverse_root(norm[:], "inv_norm")
             for c in range(Z_TILES):
                 if c % 2 == 0:
                     nc.vector.tensor_scalar_mul(out=z[:, tiles[c]], in0=z[:, tiles[c]], scalar1=inv_norm[:])
@@ -266,24 +353,185 @@ def tile_semanticaligner_w_e_kernel(
                     nc.scalar.activation(out=z[:, tiles[c]], in_=z[:, tiles[c]], func=ACT.Copy, scale=inv_norm[:])
                 nc.sync.dma_start(out=out[m][:, tiles[c]], in_=z[:, tiles[c]])
 
-        def first_linear(m, operand, after_pass):
-            banks = open_banks(H_TILES)
-            for i in range(PASSES):
-                mx_pass(m, i, operand[0], operand[1], w1_sb, w1_planes, banks)
-                after_pass(i)
-            return banks
+        def vector_sums():
+            row_sums = const.tile([P, 3], F32)
+            for at, vec in ((0, 0), (2, 1)):
+                unused = scrap.tile([P, VEC_ROW], BF16, name="unused_s", tag="scalar")
+                nc.scalar.activation(
+                    out=unused[:], in_=pair_rows[:, vec, :], func=ACT.Square, accum_out=row_sums[:, at : at + 1]
+                )
+            unused = scrap.tile([P, VEC_ROW], F32, name="unused_v", tag="vector")
+            nc.vector.scalar_tensor_tensor(
+                out=unused[:], in0=pair_rows[:, 0, :], scalar=2.0, in1=pair_rows[:, 1, :],
+                op0=ALU.mult, op1=ALU.mult, accum_out=row_sums[:, 1:2],
+            )
+            sums_psum = turn_pool.tile([P, 3], F32, name="sums_psum", tag="turn")
+            nc.tensor.matmul(out=sums_psum[:], lhsT=ones[:], rhs=row_sums[:], start=True, stop=True)
+            sums = const.tile([P, 3], F32)
+            nc.vector.tensor_copy(out=sums[:], in_=sums_psum[:])
+            return sums
 
-        def spread_gamma_beta(i):
-            if i < (VEC_ROWS - GAMMA_ROW) // Z_TILES:
-                spread_rows(GAMMA_ROW + Z_TILES * i, Z_TILES)
+        def finish_last(m, operand, vec_sums):
+            early_tiles = EARLY_COLS // N_TILE
+            parts, shift = new_parts("last")
+            early_parts = small.tile([P, 3, early_tiles], F32, name="early_parts", tag="early_parts")
+            u = z_pool.tile([P, PROJ], F32, name="u", tag="z")
+            tiles = [slice(N_TILE * c, N_TILE * (c + 1)) for c in range(Z_TILES)]
+            w_banks = [None] * Z_TILES
 
-        spread_rows(B1_ROW, MODS * H_TILES)
-        x0 = pool_over_time(0)
-        x1 = pool_over_time(1)
-        spread_rows(B2_ROW, MODS * Z_TILES)
-        z0 = gelu_and_project(0, first_linear(0, x0, spread_gamma_beta))
+            def gather(c, bank):
+                d = work.tile([P, N_TILE], F32, name="d", tag="biased")
+                shifted(m, c, bank, d[:], parts, shift)
+                nc.vector.tensor_mul(out=u[:, tiles[c]], in0=d[:], in1=spread_vec(GAMMA_AT, m, PROJ, tiles[c]))
+
+            def early_square(c):
+                sum_of_squares(u[:, tiles[c]], early_parts[:, 0, c : c + 1])
+
+            def early_product(c, at, vec):
+                product = scrap.tile([P, N_TILE], F32, name="product", tag="vector")
+                nc.vector.scalar_tensor_tensor(
+                    out=product[:], in0=u[:, tiles[c]], scalar=2.0, in1=spread_vec(vec, m, PROJ, tiles[c]),
+                    op0=ALU.mult, op1=ALU.mult, accum_out=early_parts[:, at, c : c + 1],
+                )
+
+            def copy_into_psum(c):
+                w_banks[c] = acc_pool.tile([P, N_TILE], F32, name="w%d" % c, tag="acc")
+                nc.tensor.matmul(out=w_banks[c][:], lhsT=ident_f32[:], rhs=u[:, tiles[c]], start=True, stop=False)
+
+            def gather_tile(c, bank):
+                gather(c, bank)
+                if c < early_tiles:
+                    early_square(c)
+                if c == 0:
+                    early_product(c, 1, GAMMA_AT)
+                    early_product(c, 2, BETA_AT)
+                copy_into_psum(c)
+
+            def project(first_tile, width):
+                banks = open_banks(width // N_TILE)
+                for i in range(PASSES):
+                    mx_pass(m, i, operand[0], operand[1], w2_sb, w2_planes, first_tile, banks)
+                return banks
+
+            banks = []
+            for width in W2_CHUNKS[m]:
+                if len(banks) == Z_TILES - 1:
+                    gather_tile(0, banks[0])
+                banks.extend(project(len(banks), width))
+            for c in range(1, Z_TILES):
+                gather_tile(c, banks[c])
+
+            stats, neg_var = moments(parts)
+            neg_mu = stats[:, 1:2]
+            std = stats[:, 2:3]
+            nc.scalar.activation(out=std, in_=neg_var[:], func=ACT.Sqrt, scale=-1.0, bias=ln_eps[:])
+
+            nc.vector.tensor_copy(out=factors[:, 0:2], in_=stats[:, 1:3])
+            nc.vector.tensor_sub(out=factors[:, 2:4], in0=stats[:, 1:3], in1=factors[:, 0:2])
+            early_product(1, 1, GAMMA_AT)
+            early_product(1, 2, BETA_AT)
+            factors_psum = turn_pool.tile([P, P], BF16, name="factors_psum", tag="turn")
+            nc.tensor.transpose(factors_psum[:], factors[:], ident_bf16[:])
+            factors_t = small.tile([P, P], BF16, name="factors_t", tag="factors_t")
+            nc.scalar.copy(out=factors_t[:], in_=factors_psum[:])
+            late = list(range(early_tiles, Z_TILES))
+            for c in late + list(range(early_tiles)):
+                nc.tensor.matmul(
+                    out=w_banks[c][:], lhsT=factors_t[:], rhs=scale_shift[:, tiles[c]], start=False, stop=True
+                )
+
+            three = small.tile([P, 3], F32, name="three", tag="three")
+            nc.vector.reduce_sum(out=three[:], in_=early_parts[:], axis=AXIS.X)
+            inner = small.tile([P, 2], F32, name="inner", tag="inner")
+            nc.vector.scalar_tensor_tensor(
+                out=inner[:], in0=vec_sums[:, 0:2], scalar=neg_mu, in1=three[:, 1:3], op0=ALU.mult, op1=ALU.add
+            )
+            part_mu = small.tile([P, 1], F32, name="part_mu", tag="part_mu")
+            nc.vector.scalar_tensor_tensor(
+                out=part_mu[:], in0=inner[:, 0:1], scalar=neg_mu, in1=three[:, 0:1], op0=ALU.mult, op1=ALU.add
+            )
+
+            part_std = small.tile([P, 1], F32, name="part_std", tag="part_std")
+            nc.vector.scalar_tensor_tensor(
+                out=part_std[:], in0=vec_sums[:, 2:3], scalar=std, in1=inner[:, 1:2], op0=ALU.mult, op1=ALU.add
+            )
+            square = small.tile([P, 1], F32, name="square", tag="square")
+            nc.vector.scalar_tensor_tensor(
+                out=square[:], in0=part_std[:], scalar=std, in1=part_mu[:], op0=ALU.mult, op1=ALU.add
+            )
+            floor = small.tile([P, 1], F32, name="floor", tag="floor")
+            nc.vector.tensor_scalar(
+                out=floor[:], in0=neg_var[:], scalar1=-NORM_EPS * NORM_EPS, scalar2=LN_EPS * NORM_EPS * NORM_EPS,
+                op0=ALU.mult, op1=ALU.add,
+            )
+            for c in late:
+                share = small.tile([P, 1], F32, name="share%d" % c, tag="share%d" % c)
+                sum_of_squares(w_banks[c][:], share[:])
+                total = small.tile([P, 1], F32, name="square%d" % c, tag="square%d" % c)
+                if c < late[-1]:
+                    nc.vector.tensor_add(out=total[:], in0=share[:], in1=square[:])
+                else:
+                    nc.vector.tensor_scalar(
+                        out=total[:], in0=share[:], scalar1=square[:], scalar2=floor[:], op0=ALU.add, op1=ALU.max
+                    )
+                square = total
+            norm = small.tile([P, 1], F32, name="norm", tag="norm")
+            nc.scalar.sqrt(out=norm[:], in_=square[:])
+            inv_norm = small.tile([P, 1], F32, name="inv_norm", tag="inv_norm")
+            nc.vector.reciprocal(out=inv_norm[:], in_=norm[:])
+            for c, w in enumerate(w_banks):
+                if c % 2 == 0:
+                    nc.vector.tensor_scalar_mul(out=u[:, tiles[c]], in0=w[:], scalar1=inv_norm[:])
+                else:
+                    nc.scalar.activation(out=u[:, tiles[c]], in_=w[:], func=ACT.Copy, scale=inv_norm[:])
+                nc.sync.dma_start(out=out[m][:, tiles[c]], in_=u[:, tiles[c]])
+
+        def hidden(m, x, after_range):
+            h = rows_pool.tile([P, D], BF16, name="h", tag="rows")
+            codes = operand_pool.tile([P, PASSES, P], U32, name="h_codes", tag="h_codes", align_bytes=64)
+            planes = operand_pool.tile([P, PASSES, P], U8, name="h_planes", tag="h_planes", align_bytes=64)
+
+            def bias_and_gelu(j, bank):
+                biased = work.tile([P, N_TILE], F32, name="biased", tag="biased")
+                cols = slice(N_TILE * j, N_TILE * (j + 1))
+                nc.vector.tensor_add(out=biased[:], in0=bank[:], in1=spread_vec(B1_AT, m, D, cols))
+                nc.scalar.activation(out=h[:, cols], in_=biased[:], func=ACT.Gelu)
+
+            first_tile = 0
+            for width in W1_CHUNKS[m]:
+                banks = open_banks(width // N_TILE)
+                for i in range(PASSES):
+                    mx_pass(m, i, x[0], x[1], w1_sb, w1_planes, first_tile, banks)
+                make_operand(h, codes, planes, list(enumerate(banks, first_tile)), bias_and_gelu)
+                after_range()
+                first_tile += len(banks)
+            return codes, planes
+
+        head_banks = spread_banks(B1_AT, VEC_LEN, True)
+
+        def run_next(calls):
+            if calls:
+                calls.pop(0)()
+
+        preload_table(ACT.Gelu)
+        turn_vectors()
+        for unused in range(4):
+            run_next(head_banks)
+        x0 = pool_over_time(0, lambda: run_next(head_banks))
+        x1 = pool_over_time(1, lambda: run_next(head_banks))
+        h0 = hidden(0, x0, lambda: None)
+        z0 = open_banks(Z_TILES)
+        for i in range(PASSES):
+            mx_pass(0, i, h0[0], h0[1], w2_sb, w2_planes, 0, z0)
+        vec_sums = vector_sums()
+        y0 = normalise(0, z0)
+        first_norm = []
+
+        def next_step_of_first_norm():
+            if not first_norm:
+                first_norm.extend(add_beta(0, *y0))
+
+        h1 = hidden(1, x1, next_step_of_first_norm)
         preload_table(ACT.Sqrt)
-        normalise_and_store(0, z0, ACT.Gelu)
-        z1 = gelu_and_project(1, first_linear(1, x1, lambda i: None))
-        preload_table(ACT.Sqrt)
-        normalise_and_store(1, z1, None)
+        scale_and_store(0, *first_norm)
+        finish_last(1, h1, vec_sums)

@@ -27,16 +27,16 @@ Z_TILES = PROJ // N_TILE
 PLANES_PER_SLOT = 4
 W1_CHUNKS = ((2560,), (1536, 1024))
 W2_CHUNKS = ((2048,), (1024, 512, 512))
+HEAD_PASSES = W1_CHUNKS[1][0] // K_PASS
 LN_EPS = 1e-5
 NORM_EPS = 1e-12
 
-EARLY_COLS = W2_CHUNKS[1][0]
-VEC_ROW = 2 * P
 B1_AT = 0
 B2_AT = B1_AT + MODS * D
 GAMMA_AT = B2_AT + MODS * PROJ
-BETA_AT = GAMMA_AT + MODS * PROJ
-VEC_LEN = BETA_AT + MODS * PROJ
+VEC_LEN = GAMMA_AT + MODS * PROJ
+
+assert PROJ & (PROJ - 1) == 0
 
 FLOPS = 2 * MODS * P * D * (D + PROJ)
 
@@ -76,30 +76,29 @@ def tile_semanticaligner_w_e_kernel(
 
         ident_f32 = const.tile([P, P], F32)
         make_identity(nc, ident_f32[:])
+        ident_bf16 = const.tile([P, P], BF16)
+        make_identity(nc, ident_bf16[:])
 
-        vec_rows = const.tile([P, VEC_ROW], BF16)
+        vec_rows = const.tile([P, N_TILE], BF16)
         nc.vector.memset(vec_rows[:], 0.0)
 
         slots = -(-MODS * PASSES // PLANES_PER_SLOT)
         w1_planes = const.tile([P, slots, D], U8, align_bytes=64)
         nc.vector.memset(w1_planes[:].bitcast(I32), 0)
 
-        pair_rows = const.tile([P, 2, VEC_ROW], BF16)
-        nc.vector.memset(pair_rows[:], 0.0)
-
-        scale_shift = const.tile([P, PROJ], BF16)
-        nc.vector.memset(scale_shift[:], 0.0)
-
         w2_planes = const.tile([P, slots, PROJ], U8, align_bytes=64)
         nc.vector.memset(w2_planes[:].bitcast(I32), 0)
+
+        scale_shift = const.tile([P, MODS, PROJ], BF16)
+        nc.vector.memset(scale_shift[:].rearrange("p m c -> p (m c)").bitcast(I32), 0)
 
         ln_eps = const.tile([P, 1], F32)
         nc.vector.memset(ln_eps[:], LN_EPS)
         minus_half = const.tile([P, 1], F32)
         nc.vector.memset(minus_half[:], -0.5)
-        ones = const.tile([P, P], F32)
-        nc.vector.memset(ones[:], 1.0)
-        factors = const.tile([P, P], BF16)
+        half = const.tile([P, 1], F32)
+        nc.vector.memset(half[:], 0.5)
+        factors = const.tile([P, MODS, P], BF16)
         nc.vector.memset(factors[:], 0.0)
 
         feats_sb = []
@@ -126,23 +125,18 @@ def tile_semanticaligner_w_e_kernel(
                 start += width
 
         def load_vector_rows():
-            for start, vec in ((B1_AT, b1), (B2_AT, b2), (GAMMA_AT, gamma), (BETA_AT, beta)):
-                pieces = vec.rearrange("m (j c) -> (m j) c", c=VEC_ROW)
-                first_row = start // VEC_ROW
+            for start, vec in ((B1_AT, b1), (B2_AT, b2), (GAMMA_AT, gamma)):
+                pieces = vec.rearrange("m (j c) -> (m j) c", c=N_TILE)
+                first_row = start // N_TILE
                 nc.sync.dma_start(out=vec_rows[first_row : first_row + pieces.shape[0], :], in_=pieces)
 
-        def load_last_vectors():
-            last = MODS - 1
-            for row, vec in enumerate((gamma, beta, gamma, beta)):
-                nc.sync.dma_start(out=scale_shift[row : row + 1, :], in_=vec[last : last + 1, :])
-            for at, vec in enumerate((gamma, beta)):
-                pieces = vec[last, 0:EARLY_COLS].rearrange("(j c) -> j c", c=VEC_ROW)
-                nc.sync.dma_start(out=pair_rows[0 : pieces.shape[0], at, :], in_=pieces)
+        def load_scale_shift():
+            for row, vec in ((0, gamma), (1, gamma), (2, beta), (4, beta)):
+                nc.sync.dma_start(out=scale_shift[row : row + 1, :, :], in_=vec.unsqueeze(0))
 
-        load_vector_rows()
         load_feats(0)
+        load_vector_rows()
         load_feats(1)
-        load_last_vectors()
         for planes, scales, slot in (
             (w1_planes, W1_scales, 0),
             (w1_planes, W1_scales, 1),
@@ -152,42 +146,38 @@ def tile_semanticaligner_w_e_kernel(
             (w2_planes, W2_scales, 2),
         ):
             load_scale_planes(nc, planes, scales, slot)
-        ident_bf16 = const.tile([P, P], BF16)
-        make_identity(nc, ident_bf16[:])
         for m in range(MODS):
             load_weight(m, w1_pool, W1_words, D, W1_CHUNKS[m], w1_sb, "w1")
+            if m == 0:
+                load_scale_shift()
             load_weight(m, w2_pool, W2_words, PROJ, W2_CHUNKS[m], w2_sb, "w2")
 
-        vec_words = const.tile([P, P], F32)
-
-        def turn_vectors():
-            words_psum = turn_pool.tile([P, P], F32, name="words_psum", tag="turn")
-            nc.tensor.transpose(words_psum[:], vec_rows[:].bitcast(F32), ident_f32[:])
-            nc.vector.tensor_copy(out=vec_words[:], in_=words_psum[:])
-
         spread = const.tile([P, VEC_LEN], BF16)
-        spread_words = spread[:].bitcast(F32)
-        rows_per_bank = N_TILE // P
 
         def spread_bank(first, on_scalar):
-            bank = turn_pool.tile([P, rows_per_bank, P], F32, name="bank", tag="turn")
-            for i in range(rows_per_bank):
-                nc.tensor.transpose(
-                    bank[:, i, :], vec_words[:, first + i : first + i + 1].to_broadcast([P, P]), ident_f32[:]
+            bank = turn_pool.tile([P, 2 * N_TILE], BF16, name="bank", tag="turn")
+            for i in range(2):
+                nc.tensor.matmul(
+                    out=bank[:, i * N_TILE : (i + 1) * N_TILE],
+                    lhsT=ident_bf16[:, first + i : first + i + 1].to_broadcast([P, P]),
+                    rhs=vec_rows[:],
+                    start=True,
+                    stop=True,
                 )
-            dst = spread_words[:, first * P : (first + rows_per_bank) * P]
-            src = bank[:].rearrange("p r w -> p (r w)")
+            dst = spread[:, first * N_TILE : (first + 2) * N_TILE]
             if on_scalar:
-                nc.scalar.copy(out=dst, in_=src)
+                nc.scalar.copy(out=dst, in_=bank[:])
             else:
-                nc.vector.tensor_copy(out=dst, in_=src)
+                nc.vector.tensor_copy(out=dst, in_=bank[:])
 
-        def spread_banks(start, length, share):
-            firsts = range(start // VEC_ROW, (start + length) // VEC_ROW, rows_per_bank)
-            return [
-                (lambda first=first, on_scalar=(i % 2 == 0 or not share): spread_bank(first, on_scalar))
-                for i, first in enumerate(firsts)
-            ]
+        banks_to_spread = list(range(0, VEC_LEN // N_TILE, 2))
+
+        def spread_next(count):
+            for first in banks_to_spread[0:count]:
+                spread_bank(first, on_scalar=(first // 2) % 2 == 0)
+            del_count = min(count, len(banks_to_spread))
+            for unused in range(del_count):
+                banks_to_spread.pop(0)
 
         def spread_vec(start, m, width, cols):
             return spread[:, start + m * width + cols.start : start + m * width + cols.stop]
@@ -260,233 +250,156 @@ def tile_semanticaligner_w_e_kernel(
             nc.gpsimd.tensor_tensor(out=root[:], in0=src, in1=minus_half[:], op=ALU.pow)
             return root
 
-        def sum_of_squares(src, accum):
-            squares = scrap.tile([P, N_TILE], BF16, name="squares", tag="scalar")
-            nc.scalar.activation(out=squares[:], in_=src, func=ACT.Square, accum_out=accum)
+        tiles = [slice(N_TILE * c, N_TILE * (c + 1)) for c in range(Z_TILES)]
 
-        def new_parts(name):
-            parts = small.tile([P, 2, Z_TILES], F32, name=name + "_parts", tag="parts")
-            shift = small.tile([P, 1], F32, name=name + "_shift", tag="shift")
+        def new_parts(m):
+            parts = small.tile([P, 2, Z_TILES], F32, name="parts%d" % m, tag="parts")
+            shift = small.tile([P, 1], F32, name="shift%d" % m, tag="shift")
             return parts, shift
 
-        def shifted(m, c, bank, d, parts, shift):
-            b2_tile = spread_vec(B2_AT, m, PROJ, slice(N_TILE * c, N_TILE * (c + 1)))
-            if c == 0:
-                z = work.tile([P, N_TILE], F32, name="z0", tag="biased")
-                total = small.tile([P, 1], F32, name="total0", tag="total0")
-                nc.vector.scalar_tensor_tensor(
-                    out=z[:], in0=bank[:], scalar=1.0, in1=b2_tile, op0=ALU.mult, op1=ALU.add, accum_out=total[:]
-                )
-                nc.vector.tensor_scalar_mul(out=shift[:], in0=total[:], scalar1=1.0 / N_TILE)
-                nc.vector.tensor_scalar(
-                    out=d, in0=z[:], scalar1=shift[:], scalar2=None, op0=ALU.subtract, op1=ALU.add,
-                    accum_out=parts[:, 1, c : c + 1],
-                )
-            else:
-                nc.vector.scalar_tensor_tensor(
-                    out=d, in0=bank[:], scalar=shift[:], in1=b2_tile, op0=ALU.subtract, op1=ALU.add,
-                    accum_out=parts[:, 1, c : c + 1],
-                )
-            sum_of_squares(d, parts[:, 0, c : c + 1])
+        b2_means = const.tile([P, MODS], F32)
+        b2_sums = const.tile([P, MODS], F32)
 
-        def moments(parts):
-            stats = small.tile([P, 3], F32, name="stats", tag="stats")
-            both = small.tile([P, 2], F32, name="both", tag="both")
-            nc.vector.reduce_sum(out=both[:], in_=parts[:], axis=AXIS.X)
-            nc.vector.tensor_scalar_mul(out=stats[:, 0:2], in0=both[:], scalar1=-1.0 / PROJ)
-            neg_var = small.tile([P, 1], F32, name="neg_var", tag="neg_var")
-            nc.vector.scalar_tensor_tensor(
-                out=neg_var[:], in0=stats[:, 1:2], scalar=stats[:, 1:2], in1=stats[:, 0:1], op0=ALU.mult, op1=ALU.add
-            )
-            return stats, neg_var
-
-        def normalise(m, banks):
-            tiles = [slice(N_TILE * c, N_TILE * (c + 1)) for c in range(Z_TILES)]
-            z = z_pool.tile([P, PROJ], F32, name="z", tag="z")
-            parts, shift = new_parts("first")
-            for c in range(Z_TILES):
-                shifted(m, c, banks[c], z[:, tiles[c]], parts, shift)
-            stats, neg_var = moments(parts)
-            var_eps = small.tile([P, 1], F32, name="var_eps", tag="var_eps")
-            nc.vector.tensor_scalar(
-                out=var_eps[:], in0=neg_var[:], scalar1=-1.0, scalar2=LN_EPS, op0=ALU.mult, op1=ALU.add
-            )
-            rstd = inverse_root(var_eps[:], "rstd")
-
-            nc.vector.scalar_tensor_tensor(
-                out=z[:],
-                in0=z[:],
-                scalar=stats[:, 1:2],
-                in1=spread_vec(GAMMA_AT, m, PROJ, slice(0, PROJ)),
-                op0=ALU.add,
-                op1=ALU.mult,
-            )
-            return z, rstd
-
-        def add_beta(m, z, rstd):
-            tiles = [slice(N_TILE * c, N_TILE * (c + 1)) for c in range(Z_TILES)]
-            sumsq = small.tile([P, Z_TILES], F32, name="sumsq", tag="sumsq")
-            for c in range(Z_TILES):
-                nc.vector.scalar_tensor_tensor(
-                    out=z[:, tiles[c]],
-                    in0=z[:, tiles[c]],
-                    scalar=rstd[:],
-                    in1=spread_vec(BETA_AT, m, PROJ, tiles[c]),
-                    op0=ALU.mult,
-                    op1=ALU.add,
-                )
-                square = scrap.tile([P, N_TILE], BF16, name="square", tag="scalar")
-                nc.scalar.activation(out=square[:], in_=z[:, tiles[c]], func=ACT.Square, accum_out=sumsq[:, c : c + 1])
-
-            return z, sumsq
-
-        def scale_and_store(m, z, sumsq):
-            tiles = [slice(N_TILE * c, N_TILE * (c + 1)) for c in range(Z_TILES)]
-            norm = small.tile([P, 1], F32, name="norm", tag="norm")
-            nc.vector.reduce_sum(out=norm[:], in_=sumsq[:], axis=AXIS.X)
-            nc.vector.tensor_scalar_max(out=norm[:], in0=norm[:], scalar1=NORM_EPS * NORM_EPS)
-            inv_norm = inverse_root(norm[:], "inv_norm")
-            for c in range(Z_TILES):
-                if c % 2 == 0:
-                    nc.vector.tensor_scalar_mul(out=z[:, tiles[c]], in0=z[:, tiles[c]], scalar1=inv_norm[:])
-                else:
-                    nc.scalar.activation(out=z[:, tiles[c]], in_=z[:, tiles[c]], func=ACT.Copy, scale=inv_norm[:])
-                nc.sync.dma_start(out=out[m][:, tiles[c]], in_=z[:, tiles[c]])
-
-        def vector_sums():
-            row_sums = const.tile([P, 3], F32)
-            for at, vec in ((0, 0), (2, 1)):
-                unused = scrap.tile([P, VEC_ROW], BF16, name="unused_s", tag="scalar")
+        def constants_of_norms():
+            for m in range(MODS):
+                unused = scrap.tile([P, N_TILE], BF16, name="unused_s", tag="scalar")
                 nc.scalar.activation(
-                    out=unused[:], in_=pair_rows[:, vec, :], func=ACT.Square, accum_out=row_sums[:, at : at + 1]
+                    out=unused[:], in_=spread_vec(B2_AT, m, PROJ, tiles[0]), func=ACT.Copy,
+                    accum_out=b2_sums[:, m : m + 1],
                 )
-            unused = scrap.tile([P, VEC_ROW], F32, name="unused_v", tag="vector")
-            nc.vector.scalar_tensor_tensor(
-                out=unused[:], in0=pair_rows[:, 0, :], scalar=2.0, in1=pair_rows[:, 1, :],
-                op0=ALU.mult, op1=ALU.mult, accum_out=row_sums[:, 1:2],
-            )
-            sums_psum = turn_pool.tile([P, 3], F32, name="sums_psum", tag="turn")
-            nc.tensor.matmul(out=sums_psum[:], lhsT=ones[:], rhs=row_sums[:], start=True, stop=True)
-            sums = const.tile([P, 3], F32)
-            nc.vector.tensor_copy(out=sums[:], in_=sums_psum[:])
-            return sums
+            nc.vector.tensor_scalar_mul(out=b2_means[:], in0=b2_sums[:], scalar1=1.0 / N_TILE)
+            nc.vector.tensor_scalar_mul(out=scale_shift[0:2, :, :], in0=scale_shift[0:2, :, :], scalar1=-1.0 / PROJ)
 
-        def finish_last(m, operand, vec_sums):
-            early_tiles = EARLY_COLS // N_TILE
-            parts, shift = new_parts("last")
-            early_parts = small.tile([P, 3, early_tiles], F32, name="early_parts", tag="early_parts")
-            u = z_pool.tile([P, PROJ], F32, name="u", tag="z")
-            tiles = [slice(N_TILE * c, N_TILE * (c + 1)) for c in range(Z_TILES)]
-            w_banks = [None] * Z_TILES
-
-            def gather(c, bank):
-                d = work.tile([P, N_TILE], F32, name="d", tag="biased")
-                shifted(m, c, bank, d[:], parts, shift)
-                nc.vector.tensor_mul(out=u[:, tiles[c]], in0=d[:], in1=spread_vec(GAMMA_AT, m, PROJ, tiles[c]))
-
-            def early_square(c):
-                sum_of_squares(u[:, tiles[c]], early_parts[:, 0, c : c + 1])
-
-            def early_product(c, at, vec):
-                product = scrap.tile([P, N_TILE], F32, name="product", tag="vector")
-                nc.vector.scalar_tensor_tensor(
-                    out=product[:], in0=u[:, tiles[c]], scalar=2.0, in1=spread_vec(vec, m, PROJ, tiles[c]),
-                    op0=ALU.mult, op1=ALU.mult, accum_out=early_parts[:, at, c : c + 1],
-                )
-
-            def copy_into_psum(c):
-                w_banks[c] = acc_pool.tile([P, N_TILE], F32, name="w%d" % c, tag="acc")
-                nc.tensor.matmul(out=w_banks[c][:], lhsT=ident_f32[:], rhs=u[:, tiles[c]], start=True, stop=False)
-
-            def gather_tile(c, bank):
-                gather(c, bank)
-                if c < early_tiles:
-                    early_square(c)
-                if c == 0:
-                    early_product(c, 1, GAMMA_AT)
-                    early_product(c, 2, BETA_AT)
-                copy_into_psum(c)
-
-            def project(first_tile, width):
-                banks = open_banks(width // N_TILE)
-                for i in range(PASSES):
-                    mx_pass(m, i, operand[0], operand[1], w2_sb, w2_planes, first_tile, banks)
-                return banks
-
-            banks = []
-            for width in W2_CHUNKS[m]:
-                if len(banks) == Z_TILES - 1:
-                    gather_tile(0, banks[0])
-                banks.extend(project(len(banks), width))
-            for c in range(1, Z_TILES):
-                gather_tile(c, banks[c])
-
-            stats, neg_var = moments(parts)
-            neg_mu = stats[:, 1:2]
-            std = stats[:, 2:3]
-            nc.scalar.activation(out=std, in_=neg_var[:], func=ACT.Sqrt, scale=-1.0, bias=ln_eps[:])
-
-            nc.vector.tensor_copy(out=factors[:, 0:2], in_=stats[:, 1:3])
-            nc.vector.tensor_sub(out=factors[:, 2:4], in0=stats[:, 1:3], in1=factors[:, 0:2])
-            early_product(1, 1, GAMMA_AT)
-            early_product(1, 2, BETA_AT)
-            factors_psum = turn_pool.tile([P, P], BF16, name="factors_psum", tag="turn")
-            nc.tensor.transpose(factors_psum[:], factors[:], ident_bf16[:])
-            factors_t = small.tile([P, P], BF16, name="factors_t", tag="factors_t")
-            nc.scalar.copy(out=factors_t[:], in_=factors_psum[:])
-            late = list(range(early_tiles, Z_TILES))
-            for c in late + list(range(early_tiles)):
-                nc.tensor.matmul(
-                    out=w_banks[c][:], lhsT=factors_t[:], rhs=scale_shift[:, tiles[c]], start=False, stop=True
-                )
-
-            three = small.tile([P, 3], F32, name="three", tag="three")
-            nc.vector.reduce_sum(out=three[:], in_=early_parts[:], axis=AXIS.X)
-            inner = small.tile([P, 2], F32, name="inner", tag="inner")
-            nc.vector.scalar_tensor_tensor(
-                out=inner[:], in0=vec_sums[:, 0:2], scalar=neg_mu, in1=three[:, 1:3], op0=ALU.mult, op1=ALU.add
-            )
-            part_mu = small.tile([P, 1], F32, name="part_mu", tag="part_mu")
-            nc.vector.scalar_tensor_tensor(
-                out=part_mu[:], in0=inner[:, 0:1], scalar=neg_mu, in1=three[:, 0:1], op0=ALU.mult, op1=ALU.add
-            )
-
-            part_std = small.tile([P, 1], F32, name="part_std", tag="part_std")
-            nc.vector.scalar_tensor_tensor(
-                out=part_std[:], in0=vec_sums[:, 2:3], scalar=std, in1=inner[:, 1:2], op0=ALU.mult, op1=ALU.add
-            )
-            square = small.tile([P, 1], F32, name="square", tag="square")
-            nc.vector.scalar_tensor_tensor(
-                out=square[:], in0=part_std[:], scalar=std, in1=part_mu[:], op0=ALU.mult, op1=ALU.add
-            )
-            floor = small.tile([P, 1], F32, name="floor", tag="floor")
+        def find_shift(m, bank, shift):
+            unused = scrap.tile([P, N_TILE], BF16, name="unused_s", tag="scalar")
+            total = small.tile([P, 1], F32, name="total", tag="total")
+            nc.scalar.activation(out=unused[:], in_=bank[:], func=ACT.Copy, accum_out=total[:])
             nc.vector.tensor_scalar(
-                out=floor[:], in0=neg_var[:], scalar1=-NORM_EPS * NORM_EPS, scalar2=LN_EPS * NORM_EPS * NORM_EPS,
+                out=shift[:], in0=total[:], scalar1=1.0 / N_TILE, scalar2=b2_means[:, m : m + 1],
                 op0=ALU.mult, op1=ALU.add,
             )
-            for c in late:
-                share = small.tile([P, 1], F32, name="share%d" % c, tag="share%d" % c)
-                sum_of_squares(w_banks[c][:], share[:])
-                total = small.tile([P, 1], F32, name="square%d" % c, tag="square%d" % c)
-                if c < late[-1]:
-                    nc.vector.tensor_add(out=total[:], in0=share[:], in1=square[:])
-                else:
-                    nc.vector.tensor_scalar(
-                        out=total[:], in0=share[:], scalar1=square[:], scalar2=floor[:], op0=ALU.add, op1=ALU.max
+
+        def shifted(m, c, bank, d, parts, shift):
+            nc.vector.scalar_tensor_tensor(
+                out=d, in0=bank[:], scalar=shift[:], in1=spread_vec(B2_AT, m, PROJ, tiles[c]),
+                op0=ALU.subtract, op1=ALU.add, accum_out=parts[:, 1, c : c + 1],
+            )
+            squares = scrap.tile([P, N_TILE], BF16, name="squares", tag="scalar")
+            nc.scalar.activation(
+                out=squares[:], in_=d, func=ACT.Square, scale=PROJ**0.5, accum_out=parts[:, 0, c : c + 1]
+            )
+
+        def moments(parts):
+            sums = small.tile([P, 3], F32, name="sums", tag="sums")
+            nc.vector.reduce_sum(out=sums[:, 0:2], in_=parts[:], axis=AXIS.X)
+            neg_var = small.tile([P, 1], F32, name="neg_var", tag="neg_var")
+            nc.vector.scalar_tensor_tensor(
+                out=neg_var[:], in0=sums[:, 1:2], scalar=sums[:, 1:2], in1=sums[:, 0:1],
+                op0=ALU.mult, op1=ALU.subtract,
+            )
+            return sums, neg_var
+
+        def project_range(m, operand, first_tile, width, banks, passes):
+            for i in passes:
+                mx_pass(m, i, operand[0], operand[1], w2_sb, w2_planes, first_tile, banks)
+
+        def project(m, operand, banks):
+            begun = len(banks)
+            all_banks = list(banks)
+            for r, width in enumerate(W2_CHUNKS[m]):
+                first_tile = 0 if r == 0 else len(all_banks)
+                if r > 0 or not begun:
+                    all_banks.extend(open_banks(width // N_TILE))
+                passes = range(HEAD_PASSES if r == 0 and begun else 0, PASSES)
+                project_range(m, operand, first_tile, width, all_banks[first_tile:], passes)
+            return all_banks
+
+        def gather(m, banks, after_difference):
+            u = z_pool.tile([P, PROJ], F32, name="u", tag="z")
+            parts, shift = new_parts(m)
+            find_shift(m, banks[0], shift)
+            d = [None] * Z_TILES
+            for step in range(Z_TILES + 1):
+                if step < Z_TILES:
+                    d[step] = work.tile([P, N_TILE], F32, name="d", tag="biased")
+                    shifted(m, step, banks[step], d[step][:], parts, shift)
+                    after_difference(step)
+                if step > 0:
+                    c = step - 1
+                    nc.vector.tensor_mul(out=u[:, tiles[c]], in0=d[c][:], in1=spread_vec(GAMMA_AT, m, PROJ, tiles[c]))
+            return u, parts
+
+        def deviation(m, parts):
+            sums, neg_var = moments(parts)
+            total = sums[:, 1:2]
+            std = sums[:, 2:3]
+            last = m == MODS - 1
+            if last:
+                for out_std in (std, factors[:, m, 2:3]):
+                    nc.scalar.activation(
+                        out=out_std, in_=neg_var[:], func=ACT.Sqrt, scale=-1.0 / PROJ**2, bias=ln_eps[:]
                     )
-                square = total
+            else:
+                var_eps = small.tile([P, 1], F32, name="var_eps", tag="var_eps")
+                nc.vector.tensor_scalar(
+                    out=var_eps[:], in0=neg_var[:], scalar1=-1.0 / PROJ**2, scalar2=LN_EPS, op0=ALU.mult, op1=ALU.add
+                )
+                nc.gpsimd.tensor_tensor(out=std, in0=var_eps[:], in1=half[:], op=ALU.pow)
+            nc.vector.tensor_copy(out=factors[:, m, 0:1], in_=total)
+            floor = small.tile([P, 1], F32, name="floor", tag="floor")
+            nc.vector.tensor_scalar(
+                out=floor[:], in0=neg_var[:], scalar1=-((NORM_EPS / PROJ) ** 2), scalar2=LN_EPS * NORM_EPS**2,
+                op0=ALU.mult, op1=ALU.add,
+            )
+            nc.vector.tensor_sub(out=factors[:, m, 1:2], in0=total, in1=factors[:, m, 0:1])
+            if not last:
+                nc.vector.tensor_copy(out=factors[:, m, 2:3], in_=std)
+            nc.vector.tensor_sub(out=factors[:, m, 4:5], in0=std, in1=factors[:, m, 2:3])
+            return floor
+
+        def add_row_factors(m, u, floor):
+            factors_psum = turn_pool.tile([P, P], BF16, name="factors_psum", tag="turn")
+            nc.tensor.transpose(factors_psum[:], factors[:, m, :], ident_bf16[:])
+            factors_t = small.tile([P, P], BF16, name="factors_t", tag="factors_t")
+            nc.scalar.copy(out=factors_t[:], in_=factors_psum[:])
+            sumsq = small.tile([P, Z_TILES], F32, name="sumsq", tag="sumsq")
+            for c in range(Z_TILES):
+                bank = acc_pool.tile([P, N_TILE], F32, name="rows%d" % c, tag="acc")
+                nc.tensor.matmul(
+                    out=bank[:], lhsT=factors_t[:], rhs=scale_shift[:, m, tiles[c]], start=True, stop=True
+                )
+                nc.vector.tensor_add(out=u[:, tiles[c]], in0=bank[:], in1=u[:, tiles[c]])
+                squares = scrap.tile([P, N_TILE], BF16, name="squares", tag="scalar")
+                nc.scalar.activation(
+                    out=squares[:], in_=u[:, tiles[c]], func=ACT.Square, accum_out=sumsq[:, c : c + 1]
+                )
+            most = small.tile([P, 1], F32, name="most", tag="most")
+            nc.vector.reduce_sum(out=most[:], in_=sumsq[:, 0 : Z_TILES - 1], axis=AXIS.X)
+            square = small.tile([P, 1], F32, name="square", tag="square")
+            nc.vector.tensor_scalar(
+                out=square[:], in0=sumsq[:, Z_TILES - 1 : Z_TILES], scalar1=most[:], scalar2=floor[:],
+                op0=ALU.add, op1=ALU.max,
+            )
+            return square
+
+        def inverse_norm(m, square):
+            if m < MODS - 1:
+                return inverse_root(square[:], "inv_norm")
             norm = small.tile([P, 1], F32, name="norm", tag="norm")
             nc.scalar.sqrt(out=norm[:], in_=square[:])
             inv_norm = small.tile([P, 1], F32, name="inv_norm", tag="inv_norm")
             nc.vector.reciprocal(out=inv_norm[:], in_=norm[:])
-            for c, w in enumerate(w_banks):
-                if c % 2 == 0:
-                    nc.vector.tensor_scalar_mul(out=u[:, tiles[c]], in0=w[:], scalar1=inv_norm[:])
-                else:
-                    nc.scalar.activation(out=u[:, tiles[c]], in_=w[:], func=ACT.Copy, scale=inv_norm[:])
-                nc.sync.dma_start(out=out[m][:, tiles[c]], in_=u[:, tiles[c]])
+            return inv_norm
 
-        def hidden(m, x, after_range):
+        def scale_and_store(m, w, inv_norm):
+            for c in range(Z_TILES):
+                if c == 1:
+                    nc.scalar.activation(out=w[:, tiles[c]], in_=w[:, tiles[c]], func=ACT.Copy, scale=inv_norm[:])
+                else:
+                    nc.vector.tensor_scalar_mul(out=w[:, tiles[c]], in0=w[:, tiles[c]], scalar1=inv_norm[:])
+                nc.sync.dma_start(out=out[m][:, tiles[c]], in_=w[:, tiles[c]])
+
+        def hidden(m, x, after_pass, after_range, before_last):
             h = rows_pool.tile([P, D], BF16, name="h", tag="rows")
             codes = operand_pool.tile([P, PASSES, P], U32, name="h_codes", tag="h_codes", align_bytes=64)
             planes = operand_pool.tile([P, PASSES, P], U8, name="h_planes", tag="h_planes", align_bytes=64)
@@ -502,36 +415,39 @@ def tile_semanticaligner_w_e_kernel(
                 banks = open_banks(width // N_TILE)
                 for i in range(PASSES):
                     mx_pass(m, i, x[0], x[1], w1_sb, w1_planes, first_tile, banks)
+                    if i < PASSES - 1:
+                        after_pass()
+                if first_tile > 0:
+                    before_last((codes, planes))
                 make_operand(h, codes, planes, list(enumerate(banks, first_tile)), bias_and_gelu)
                 after_range()
                 first_tile += len(banks)
             return codes, planes
 
-        head_banks = spread_banks(B1_AT, VEC_LEN, True)
-
-        def run_next(calls):
-            if calls:
-                calls.pop(0)()
-
         preload_table(ACT.Gelu)
-        turn_vectors()
-        for unused in range(4):
-            run_next(head_banks)
-        x0 = pool_over_time(0, lambda: run_next(head_banks))
-        x1 = pool_over_time(1, lambda: run_next(head_banks))
-        h0 = hidden(0, x0, lambda: None)
-        z0 = open_banks(Z_TILES)
-        for i in range(PASSES):
-            mx_pass(0, i, h0[0], h0[1], w2_sb, w2_planes, 0, z0)
-        vec_sums = vector_sums()
-        y0 = normalise(0, z0)
-        first_norm = []
+        x0 = pool_over_time(0, lambda: None)
+        spread_next(5)
+        x1 = pool_over_time(1, lambda: None)
+        h0 = hidden(0, x0, lambda: spread_next(2), lambda: None, None)
+        constants_of_norms()
+        u0, parts0 = gather(0, project(0, h0, []), lambda c: None)
+        floor0 = deviation(0, parts0)
 
-        def next_step_of_first_norm():
-            if not first_norm:
-                first_norm.extend(add_beta(0, *y0))
+        inv_norms = []
+        first_banks = []
 
-        h1 = hidden(1, x1, next_step_of_first_norm)
-        preload_table(ACT.Sqrt)
-        scale_and_store(0, *first_norm)
-        finish_last(1, h1, vec_sums)
+        def norm_of_first():
+            if not inv_norms:
+                inv_norms.append(inverse_norm(0, add_row_factors(0, u0, floor0)))
+
+        def head_of_projection(operand):
+            first_banks.extend(open_banks(W2_CHUNKS[1][0] // N_TILE))
+            project_range(1, operand, 0, W2_CHUNKS[1][0], first_banks, range(HEAD_PASSES))
+
+        h1 = hidden(1, x1, lambda: None, norm_of_first, head_of_projection)
+        scale_and_store(0, u0, inv_norms[0])
+        z1 = project(1, h1, first_banks)
+
+        u1, parts1 = gather(1, z1, lambda c: preload_table(ACT.Sqrt) if c == 0 else None)
+        floor1 = deviation(1, parts1)
+        scale_and_store(1, u1, inverse_norm(1, add_row_factors(1, u1, floor1)))

@@ -94,10 +94,6 @@ def tile_semanticaligner_w_e_kernel(
 
         ln_eps = const.tile([P, 1], F32)
         nc.vector.memset(ln_eps[:], LN_EPS)
-        minus_half = const.tile([P, 1], F32)
-        nc.vector.memset(minus_half[:], -0.5)
-        half = const.tile([P, 1], F32)
-        nc.vector.memset(half[:], 0.5)
         factors = const.tile([P, MODS, P], BF16)
         nc.vector.memset(factors[:], 0.0)
 
@@ -245,11 +241,6 @@ def tile_semanticaligner_w_e_kernel(
             unused = small.tile([P, 1], F32, name="unused", tag="unused")
             nc.scalar.activation(out=unused[:], in_=ln_eps[:], func=func)
 
-        def inverse_root(src, name):
-            root = small.tile([P, 1], F32, name=name, tag=name)
-            nc.gpsimd.tensor_tensor(out=root[:], in0=src, in1=minus_half[:], op=ALU.pow)
-            return root
-
         tiles = [slice(N_TILE * c, N_TILE * (c + 1)) for c in range(Z_TILES)]
 
         def new_parts(m):
@@ -314,7 +305,7 @@ def tile_semanticaligner_w_e_kernel(
                 project_range(m, operand, first_tile, width, all_banks[first_tile:], passes)
             return all_banks
 
-        def gather(m, banks, after_difference):
+        def gather(m, banks):
             u = z_pool.tile([P, PROJ], F32, name="u", tag="z")
             parts, shift = new_parts(m)
             find_shift(m, banks[0], shift)
@@ -323,7 +314,6 @@ def tile_semanticaligner_w_e_kernel(
                 if step < Z_TILES:
                     d[step] = work.tile([P, N_TILE], F32, name="d", tag="biased")
                     shifted(m, step, banks[step], d[step][:], parts, shift)
-                    after_difference(step)
                 if step > 0:
                     c = step - 1
                     nc.vector.tensor_mul(out=u[:, tiles[c]], in0=d[c][:], in1=spread_vec(GAMMA_AT, m, PROJ, tiles[c]))
@@ -333,18 +323,8 @@ def tile_semanticaligner_w_e_kernel(
             sums, neg_var = moments(parts)
             total = sums[:, 1:2]
             std = sums[:, 2:3]
-            last = m == MODS - 1
-            if last:
-                for out_std in (std, factors[:, m, 2:3]):
-                    nc.scalar.activation(
-                        out=out_std, in_=neg_var[:], func=ACT.Sqrt, scale=-1.0 / PROJ**2, bias=ln_eps[:]
-                    )
-            else:
-                var_eps = small.tile([P, 1], F32, name="var_eps", tag="var_eps")
-                nc.vector.tensor_scalar(
-                    out=var_eps[:], in0=neg_var[:], scalar1=-1.0 / PROJ**2, scalar2=LN_EPS, op0=ALU.mult, op1=ALU.add
-                )
-                nc.gpsimd.tensor_tensor(out=std, in0=var_eps[:], in1=half[:], op=ALU.pow)
+            for out_std in (std, factors[:, m, 2:3]):
+                nc.scalar.activation(out=out_std, in_=neg_var[:], func=ACT.Sqrt, scale=-1.0 / PROJ**2, bias=ln_eps[:])
             nc.vector.tensor_copy(out=factors[:, m, 0:1], in_=total)
             floor = small.tile([P, 1], F32, name="floor", tag="floor")
             nc.vector.tensor_scalar(
@@ -352,8 +332,6 @@ def tile_semanticaligner_w_e_kernel(
                 op0=ALU.mult, op1=ALU.add,
             )
             nc.vector.tensor_sub(out=factors[:, m, 1:2], in0=total, in1=factors[:, m, 0:1])
-            if not last:
-                nc.vector.tensor_copy(out=factors[:, m, 2:3], in_=std)
             nc.vector.tensor_sub(out=factors[:, m, 4:5], in0=std, in1=factors[:, m, 2:3])
             return floor
 
@@ -382,18 +360,16 @@ def tile_semanticaligner_w_e_kernel(
             )
             return square
 
-        def inverse_norm(m, square):
-            if m < MODS - 1:
-                return inverse_root(square[:], "inv_norm")
+        def inverse_norm(square):
             norm = small.tile([P, 1], F32, name="norm", tag="norm")
             nc.scalar.sqrt(out=norm[:], in_=square[:])
             inv_norm = small.tile([P, 1], F32, name="inv_norm", tag="inv_norm")
             nc.vector.reciprocal(out=inv_norm[:], in_=norm[:])
             return inv_norm
 
-        def scale_and_store(m, w, inv_norm):
-            for c in range(Z_TILES):
-                if c == 1:
+        def scale_and_store(m, w, inv_norm, which, scalar_tile=None):
+            for c in which:
+                if c == scalar_tile:
                     nc.scalar.activation(out=w[:, tiles[c]], in_=w[:, tiles[c]], func=ACT.Copy, scale=inv_norm[:])
                 else:
                     nc.vector.tensor_scalar_mul(out=w[:, tiles[c]], in0=w[:, tiles[c]], scalar1=inv_norm[:])
@@ -430,24 +406,28 @@ def tile_semanticaligner_w_e_kernel(
         x1 = pool_over_time(1, lambda: None)
         h0 = hidden(0, x0, lambda: spread_next(2), lambda: None, None)
         constants_of_norms()
-        u0, parts0 = gather(0, project(0, h0, []), lambda c: None)
+        preload_table(ACT.Sqrt)
+        u0, parts0 = gather(0, project(0, h0, []))
         floor0 = deviation(0, parts0)
+        preload_table(ACT.Gelu)
 
-        inv_norms = []
+        squares = []
         first_banks = []
 
         def norm_of_first():
-            if not inv_norms:
-                inv_norms.append(inverse_norm(0, add_row_factors(0, u0, floor0)))
+            if not squares:
+                squares.append(add_row_factors(0, u0, floor0))
 
         def head_of_projection(operand):
             first_banks.extend(open_banks(W2_CHUNKS[1][0] // N_TILE))
             project_range(1, operand, 0, W2_CHUNKS[1][0], first_banks, range(HEAD_PASSES))
 
         h1 = hidden(1, x1, lambda: None, norm_of_first, head_of_projection)
-        scale_and_store(0, u0, inv_norms[0])
         z1 = project(1, h1, first_banks)
 
-        u1, parts1 = gather(1, z1, lambda c: preload_table(ACT.Sqrt) if c == 0 else None)
+        preload_table(ACT.Sqrt)
+        inv_norm0 = inverse_norm(squares[0])
+        u1, parts1 = gather(1, z1)
         floor1 = deviation(1, parts1)
-        scale_and_store(1, u1, inverse_norm(1, add_row_factors(1, u1, floor1)))
+        scale_and_store(0, u0, inv_norm0, range(Z_TILES))
+        scale_and_store(1, u1, inverse_norm(add_row_factors(1, u1, floor1)), range(Z_TILES), scalar_tile=1)

@@ -27,7 +27,7 @@ Z_TILES = PROJ // N_TILE
 PLANES_PER_SLOT = 4
 W1_CHUNKS = ((2560,), (1536, 1024))
 W2_CHUNKS = ((2048,), (1024, 512, 512))
-HEAD_PASSES = W1_CHUNKS[1][0] // K_PASS
+HEAD_PASSES = 2
 LN_EPS = 1e-5
 NORM_EPS = 1e-12
 
@@ -192,34 +192,34 @@ def tile_semanticaligner_w_e_kernel(
             )
             return grouped
 
-        def make_operand(rows, codes, planes, tiles, fill, after_step=lambda: None):
-            grouped = []
-            for step in range(len(tiles) + 2 if tiles else 0):
-                if step < len(tiles):
-                    fill(*tiles[step])
-                if 1 <= step <= len(tiles):
-                    grouped.append(turn_pass(rows, tiles[step - 1][0]))
-                if step >= 2:
-                    g = tiles[step - 2][0]
-                    nc.vector.quantize_mx(
-                        out=codes[:, g, :].bitcast(FP8X4), scales=planes[:, g, :], in_=grouped[step - 2][:]
-                    )
-                after_step()
-
-        def pool_over_time(m, after_step):
-            pooled = rows_pool.tile([P, D], BF16, name="pooled", tag="rows")
-
-            codes = operand_pool.tile([P, PASSES, P], U32, name="x_codes", tag="x_codes", align_bytes=64)
-            planes = operand_pool.tile([P, PASSES, P], U8, name="x_planes", tag="x_planes", align_bytes=64)
-
-            def mean_of_steps(g):
-                cols = slice(g * K_PASS, (g + 1) * K_PASS)
-                total = work.tile([P, K_PASS], BF16, name="total", tag="total")
-                nc.vector.tensor_add(out=total[:], in0=feats_sb[m][:, 0, cols], in1=feats_sb[m][:, 1, cols])
-                nc.vector.tensor_scalar_mul(out=pooled[:, cols], in0=total[:], scalar1=1.0 / STEPS)
-
-            make_operand(pooled, codes, planes, [(g,) for g in range(PASSES)], mean_of_steps, after_step)
+        def new_operand(kind):
+            codes = operand_pool.tile([P, PASSES, P], U32, name=kind + "_codes", tag=kind + "_codes", align_bytes=64)
+            planes = operand_pool.tile([P, PASSES, P], U8, name=kind + "_planes", tag=kind + "_planes", align_bytes=64)
             return codes, planes
+
+        def quantise_pass(operand, g, grouped):
+            codes, planes = operand
+            nc.vector.quantize_mx(out=codes[:, g, :].bitcast(FP8X4), scales=planes[:, g, :], in_=grouped[:])
+
+        def make_operand(rows, operand, passes, fill, after_fill=lambda: None):
+            grouped = {}
+            for step in range(len(passes) + 2):
+                if step < len(passes):
+                    fill(passes[step])
+                    if step == len(passes) - 1:
+                        after_fill()
+                if 1 <= step <= len(passes):
+                    g = passes[step - 1]
+                    grouped[g] = turn_pass(rows, g)
+                if step >= 2:
+                    g = passes[step - 2]
+                    quantise_pass(operand, g, grouped[g])
+
+        def mean_of_steps(m, pooled, g):
+            cols = slice(g * K_PASS, (g + 1) * K_PASS)
+            total = work.tile([P, K_PASS], BF16, name="total", tag="total")
+            nc.vector.tensor_add(out=total[:], in0=feats_sb[m][:, 0, cols], in1=feats_sb[m][:, 1, cols])
+            nc.vector.tensor_scalar_mul(out=pooled[:, cols], in0=total[:], scalar1=1.0 / STEPS)
 
         def open_banks(n_tiles):
             return [acc_pool.tile([P, N_TILE], F32, name="acc%d" % j, tag="acc") for j in range(n_tiles)]
@@ -377,57 +377,70 @@ def tile_semanticaligner_w_e_kernel(
 
         def hidden(m, x, after_pass, after_range, before_last):
             h = rows_pool.tile([P, D], BF16, name="h", tag="rows")
-            codes = operand_pool.tile([P, PASSES, P], U32, name="h_codes", tag="h_codes", align_bytes=64)
-            planes = operand_pool.tile([P, PASSES, P], U8, name="h_planes", tag="h_planes", align_bytes=64)
+            operand = new_operand("h")
+            all_banks = []
 
-            def bias_and_gelu(j, bank):
+            def bias_and_gelu(j):
                 biased = work.tile([P, N_TILE], F32, name="biased", tag="biased")
                 cols = slice(N_TILE * j, N_TILE * (j + 1))
-                nc.vector.tensor_add(out=biased[:], in0=bank[:], in1=spread_vec(B1_AT, m, D, cols))
+                nc.vector.tensor_add(out=biased[:], in0=all_banks[j][:], in1=spread_vec(B1_AT, m, D, cols))
                 nc.scalar.activation(out=h[:, cols], in_=biased[:], func=ACT.Gelu)
 
-            first_tile = 0
-            for width in W1_CHUNKS[m]:
-                banks = open_banks(width // N_TILE)
+            for r, width in enumerate(W1_CHUNKS[m]):
+                first_tile = len(all_banks)
+                all_banks.extend(open_banks(width // N_TILE))
                 for i in range(PASSES):
-                    mx_pass(m, i, x[0], x[1], w1_sb, w1_planes, first_tile, banks)
-                    if i < PASSES - 1:
-                        after_pass()
-                if first_tile > 0:
-                    before_last((codes, planes))
-                make_operand(h, codes, planes, list(enumerate(banks, first_tile)), bias_and_gelu)
-                after_range()
-                first_tile += len(banks)
-            return codes, planes
+                    mx_pass(m, i, x[0], x[1], w1_sb, w1_planes, first_tile, all_banks[first_tile:])
+                    after_pass(i)
+                last = r > 0
+                if last:
+                    before_last(operand)
+                make_operand(
+                    h, operand, list(range(first_tile, len(all_banks))), bias_and_gelu,
+                    after_fill=lambda: preload_table(ACT.Sqrt) if last or len(W1_CHUNKS[m]) == 1 else None,
+                )
+                if not last:
+                    after_range()
+            return operand
 
         preload_table(ACT.Gelu)
-        x0 = pool_over_time(0, lambda: None)
-        spread_next(5)
-        x1 = pool_over_time(1, lambda: None)
-        h0 = hidden(0, x0, lambda: spread_next(2), lambda: None, None)
+        pooled = [rows_pool.tile([P, D], BF16, name="pooled%d" % m, tag="rows") for m in range(MODS)]
+        x = [new_operand("x") for m in range(MODS)]
+        all_passes = list(range(PASSES))
+
+        def fill_first(g):
+            mean_of_steps(0, pooled[0], g)
+            if g > 0:
+                spread_next(1)
+
+        make_operand(pooled[0], x[0], all_passes, fill_first)
+        for g in all_passes:
+            mean_of_steps(1, pooled[1], g)
+
+        def between_passes(i):
+            if i == 1:
+                make_operand(pooled[1], x[1], all_passes, lambda g: None)
+            elif i < PASSES - 1:
+                spread_next(3)
+
+        h0 = hidden(0, x[0], between_passes, lambda: None, None)
         constants_of_norms()
-        preload_table(ACT.Sqrt)
         u0, parts0 = gather(0, project(0, h0, []))
         floor0 = deviation(0, parts0)
         preload_table(ACT.Gelu)
 
-        squares = []
         first_banks = []
-
-        def norm_of_first():
-            if not squares:
-                squares.append(add_row_factors(0, u0, floor0))
 
         def head_of_projection(operand):
             first_banks.extend(open_banks(W2_CHUNKS[1][0] // N_TILE))
             project_range(1, operand, 0, W2_CHUNKS[1][0], first_banks, range(HEAD_PASSES))
 
-        h1 = hidden(1, x1, lambda: None, norm_of_first, head_of_projection)
-        z1 = project(1, h1, first_banks)
-
-        preload_table(ACT.Sqrt)
+        squares = []
+        h1 = hidden(
+            1, x[1], lambda i: None, lambda: squares.append(add_row_factors(0, u0, floor0)), head_of_projection
+        )
         inv_norm0 = inverse_norm(squares[0])
-        u1, parts1 = gather(1, z1)
+        u1, parts1 = gather(1, project(1, h1, first_banks))
         floor1 = deviation(1, parts1)
         scale_and_store(0, u0, inv_norm0, range(Z_TILES))
         scale_and_store(1, u1, inverse_norm(add_row_factors(1, u1, floor1)), range(Z_TILES), scalar_tile=1)

@@ -25,9 +25,6 @@ PASSES = D // K_PASS
 H_TILES = D // N_TILE
 Z_TILES = PROJ // N_TILE
 PLANES_PER_SLOT = 4
-W1_CHUNKS = ((2560,), (1536, 1024))
-W2_CHUNKS = ((2048,), (1024, 512, 512))
-HEAD_PASSES = 2
 LN_EPS = 1e-5
 NORM_EPS = 1e-12
 
@@ -65,7 +62,7 @@ def tile_semanticaligner_w_e_kernel(
         w2_pool = ctx.enter_context(tc.tile_pool(name="w2", bufs=6))
         rows_pool = ctx.enter_context(tc.tile_pool(name="rows", bufs=2))
         operand_pool = ctx.enter_context(tc.tile_pool(name="operand", bufs=2))
-        work = ctx.enter_context(tc.tile_pool(name="work", bufs=3))
+        work = ctx.enter_context(tc.tile_pool(name="work", bufs=4))
         scrap = ctx.enter_context(tc.tile_pool(name="scrap", bufs=2))
         z_pool = ctx.enter_context(tc.tile_pool(name="z", bufs=2))
         small = ctx.enter_context(tc.tile_pool(name="small", bufs=2))
@@ -106,19 +103,16 @@ def tile_semanticaligner_w_e_kernel(
             nc.sync.dma_start(out=f[:], in_=feats[m])
             feats_sb.append(f)
 
-        def load_weight(m, pool, words, n_cols, chunks, kept, kind):
-            passes = range(m * PASSES, (m + 1) * PASSES)
-            start = 0
-            for width in chunks:
-                part = slice(PACK * start, PACK * (start + width))
-                for g in passes:
-                    if start == 0:
-                        kept.append(
-                            pool.tile([P, PACK * n_cols], U8, name="%s_%d" % (kind, g), tag=kind, align_bytes=64)
-                        )
-                    flat = words[g].rearrange("p n t -> p (n t)")
-                    nc.sync.dma_start(out=kept[g][:, part].bitcast(I32), in_=flat[:, part].bitcast(I32))
-                start += width
+        def load_weight(m, pool, words, n_cols, kept, kind, tapered=False):
+            for g in range(m * PASSES, (m + 1) * PASSES):
+                w = pool.tile([P, PACK * n_cols], U8, name="%s_%d" % (kind, g), tag=kind, align_bytes=64)
+                flat = words[g].rearrange("p n t -> p (n t)")
+                last = g == (m + 1) * PASSES - 1
+                width = N_TILE if tapered and last else n_cols
+                for start in range(0, n_cols, width):
+                    part = slice(PACK * start, PACK * (start + width))
+                    nc.sync.dma_start(out=w[:, part].bitcast(I32), in_=flat[:, part].bitcast(I32))
+                kept.append(w)
 
         def load_vector_rows():
             for start, vec in ((B1_AT, b1), (B2_AT, b2), (GAMMA_AT, gamma)):
@@ -128,7 +122,7 @@ def tile_semanticaligner_w_e_kernel(
 
         def load_scale_shift():
             for row, vec in ((0, gamma), (1, gamma), (2, beta), (4, beta)):
-                nc.sync.dma_start(out=scale_shift[row : row + 1, :, :], in_=vec.unsqueeze(0))
+                nc.gpsimd.dma_start(out=scale_shift[row : row + 1, :, :], in_=vec.unsqueeze(0))
 
         load_feats(0)
         load_vector_rows()
@@ -142,11 +136,10 @@ def tile_semanticaligner_w_e_kernel(
             (w2_planes, W2_scales, 2),
         ):
             load_scale_planes(nc, planes, scales, slot)
+        load_scale_shift()
         for m in range(MODS):
-            load_weight(m, w1_pool, W1_words, D, W1_CHUNKS[m], w1_sb, "w1")
-            if m == 0:
-                load_scale_shift()
-            load_weight(m, w2_pool, W2_words, PROJ, W2_CHUNKS[m], w2_sb, "w2")
+            load_weight(m, w1_pool, W1_words, D, w1_sb, "w1")
+            load_weight(m, w2_pool, W2_words, PROJ, w2_sb, "w2", tapered=m == MODS - 1)
 
         spread = const.tile([P, VEC_LEN], BF16)
 
@@ -201,19 +194,21 @@ def tile_semanticaligner_w_e_kernel(
             codes, planes = operand
             nc.vector.quantize_mx(out=codes[:, g, :].bitcast(FP8X4), scales=planes[:, g, :], in_=grouped[:])
 
-        def make_operand(rows, operand, passes, fill, after_fill=lambda: None):
+        def make_operand(rows, operand, passes, fill, use=None, after_fill=None):
             grouped = {}
-            for step in range(len(passes) + 2):
+            for step in range(len(passes) + 3):
                 if step < len(passes):
                     fill(passes[step])
-                    if step == len(passes) - 1:
+                    if step == len(passes) - 1 and after_fill:
                         after_fill()
                 if 1 <= step <= len(passes):
                     g = passes[step - 1]
                     grouped[g] = turn_pass(rows, g)
-                if step >= 2:
+                if 2 <= step <= len(passes) + 1:
                     g = passes[step - 2]
                     quantise_pass(operand, g, grouped[g])
+                if step >= 3 and use:
+                    use(passes[step - 3])
 
         def mean_of_steps(m, pooled, g):
             cols = slice(g * K_PASS, (g + 1) * K_PASS)
@@ -290,36 +285,24 @@ def tile_semanticaligner_w_e_kernel(
             )
             return sums, neg_var
 
-        def project_range(m, operand, first_tile, width, banks, passes):
-            for i in passes:
-                mx_pass(m, i, operand[0], operand[1], w2_sb, w2_planes, first_tile, banks)
-
-        def project(m, operand, banks):
-            begun = len(banks)
-            all_banks = list(banks)
-            for r, width in enumerate(W2_CHUNKS[m]):
-                first_tile = 0 if r == 0 else len(all_banks)
-                if r > 0 or not begun:
-                    all_banks.extend(open_banks(width // N_TILE))
-                passes = range(HEAD_PASSES if r == 0 and begun else 0, PASSES)
-                project_range(m, operand, first_tile, width, all_banks[first_tile:], passes)
-            return all_banks
-
         def gather(m, banks):
             u = z_pool.tile([P, PROJ], F32, name="u", tag="z")
             parts, shift = new_parts(m)
             find_shift(m, banks[0], shift)
-            d = [None] * Z_TILES
-            for step in range(Z_TILES + 1):
-                if step < Z_TILES:
-                    d[step] = work.tile([P, N_TILE], F32, name="d", tag="biased")
-                    shifted(m, step, banks[step], d[step][:], parts, shift)
-                if step > 0:
-                    c = step - 1
-                    nc.vector.tensor_mul(out=u[:, tiles[c]], in0=d[c][:], in1=spread_vec(GAMMA_AT, m, PROJ, tiles[c]))
-            return u, parts
+            differences = [work.tile([P, N_TILE], F32, name="d%d" % c, tag="biased") for c in range(Z_TILES)]
+            for c, d in enumerate(differences):
+                shifted(m, c, banks[c], d[:], parts, shift)
+            products = [
+                lambda c=c, d=d: nc.vector.tensor_mul(
+                    out=u[:, tiles[c]], in0=d[:], in1=spread_vec(GAMMA_AT, m, PROJ, tiles[c])
+                )
+                for c, d in enumerate(differences)
+            ]
+            return u, parts, products
 
-        def deviation(m, parts):
+        def deviation(m, parts, products):
+            for product in products[0:2]:
+                product()
             sums, neg_var = moments(parts)
             total = sums[:, 1:2]
             std = sums[:, 2:3]
@@ -333,6 +316,8 @@ def tile_semanticaligner_w_e_kernel(
             )
             nc.vector.tensor_sub(out=factors[:, m, 1:2], in0=total, in1=factors[:, m, 0:1])
             nc.vector.tensor_sub(out=factors[:, m, 4:5], in0=std, in1=factors[:, m, 2:3])
+            for product in products[2:]:
+                product()
             return floor
 
         def add_row_factors(m, u, floor):
@@ -342,7 +327,7 @@ def tile_semanticaligner_w_e_kernel(
             nc.scalar.copy(out=factors_t[:], in_=factors_psum[:])
             sumsq = small.tile([P, Z_TILES], F32, name="sumsq", tag="sumsq")
             for c in range(Z_TILES):
-                bank = acc_pool.tile([P, N_TILE], F32, name="rows%d" % c, tag="acc")
+                bank = turn_pool.tile([P, N_TILE], F32, name="rows%d" % c, tag="turn")
                 nc.tensor.matmul(
                     out=bank[:], lhsT=factors_t[:], rhs=scale_shift[:, m, tiles[c]], start=True, stop=True
                 )
@@ -375,33 +360,30 @@ def tile_semanticaligner_w_e_kernel(
                     nc.vector.tensor_scalar_mul(out=w[:, tiles[c]], in0=w[:, tiles[c]], scalar1=inv_norm[:])
                 nc.sync.dma_start(out=out[m][:, tiles[c]], in_=w[:, tiles[c]])
 
-        def hidden(m, x, after_pass, after_range, before_last):
+        def two_linears(m, x, after_pass):
+            s_banks = open_banks(H_TILES)
+            for i in range(PASSES):
+                mx_pass(m, i, x[0], x[1], w1_sb, w1_planes, 0, s_banks)
+                after_pass(i)
             h = rows_pool.tile([P, D], BF16, name="h", tag="rows")
             operand = new_operand("h")
-            all_banks = []
+            z_banks = []
 
             def bias_and_gelu(j):
                 biased = work.tile([P, N_TILE], F32, name="biased", tag="biased")
                 cols = slice(N_TILE * j, N_TILE * (j + 1))
-                nc.vector.tensor_add(out=biased[:], in0=all_banks[j][:], in1=spread_vec(B1_AT, m, D, cols))
+                nc.vector.tensor_add(out=biased[:], in0=s_banks[j][:], in1=spread_vec(B1_AT, m, D, cols))
                 nc.scalar.activation(out=h[:, cols], in_=biased[:], func=ACT.Gelu)
 
-            for r, width in enumerate(W1_CHUNKS[m]):
-                first_tile = len(all_banks)
-                all_banks.extend(open_banks(width // N_TILE))
-                for i in range(PASSES):
-                    mx_pass(m, i, x[0], x[1], w1_sb, w1_planes, first_tile, all_banks[first_tile:])
-                    after_pass(i)
-                last = r > 0
-                if last:
-                    before_last(operand)
-                make_operand(
-                    h, operand, list(range(first_tile, len(all_banks))), bias_and_gelu,
-                    after_fill=lambda: preload_table(ACT.Sqrt) if last or len(W1_CHUNKS[m]) == 1 else None,
-                )
-                if not last:
-                    after_range()
-            return operand
+            def project(i):
+                if i == 0:
+                    z_banks.extend(open_banks(Z_TILES))
+                mx_pass(m, i, operand[0], operand[1], w2_sb, w2_planes, 0, z_banks)
+
+            make_operand(
+                h, operand, all_passes, bias_and_gelu, use=project, after_fill=lambda: preload_table(ACT.Sqrt)
+            )
+            return z_banks
 
         preload_table(ACT.Gelu)
         pooled = [rows_pool.tile([P, D], BF16, name="pooled%d" % m, tag="rows") for m in range(MODS)]
@@ -423,24 +405,13 @@ def tile_semanticaligner_w_e_kernel(
             elif i < PASSES - 1:
                 spread_next(3)
 
-        h0 = hidden(0, x[0], between_passes, lambda: None, None)
+        z0 = two_linears(0, x[0], between_passes)
         constants_of_norms()
-        u0, parts0 = gather(0, project(0, h0, []))
-        floor0 = deviation(0, parts0)
+        u0, parts0, products0 = gather(0, z0)
+        floor0 = deviation(0, parts0, products0)
+        scale_and_store(0, u0, inverse_norm(add_row_factors(0, u0, floor0)), range(Z_TILES))
         preload_table(ACT.Gelu)
-
-        first_banks = []
-
-        def head_of_projection(operand):
-            first_banks.extend(open_banks(W2_CHUNKS[1][0] // N_TILE))
-            project_range(1, operand, 0, W2_CHUNKS[1][0], first_banks, range(HEAD_PASSES))
-
-        squares = []
-        h1 = hidden(
-            1, x[1], lambda i: None, lambda: squares.append(add_row_factors(0, u0, floor0)), head_of_projection
-        )
-        inv_norm0 = inverse_norm(squares[0])
-        u1, parts1 = gather(1, project(1, h1, first_banks))
-        floor1 = deviation(1, parts1)
-        scale_and_store(0, u0, inv_norm0, range(Z_TILES))
+        z1 = two_linears(1, x[1], lambda i: None)
+        u1, parts1, products1 = gather(1, z1)
+        floor1 = deviation(1, parts1, products1)
         scale_and_store(1, u1, inverse_norm(add_row_factors(1, u1, floor1)), range(Z_TILES), scalar_tile=1)

@@ -25,15 +25,15 @@ PASSES = D // K_PASS
 H_TILES = D // N_TILE
 Z_TILES = PROJ // N_TILE
 PLANES_PER_SLOT = 4
+W2_RANGES = ((PROJ,), (N_TILE, PROJ - N_TILE))
 LN_EPS = 1e-5
 NORM_EPS = 1e-12
 
 B1_AT = 0
 B2_AT = B1_AT + MODS * D
 GAMMA_AT = B2_AT + MODS * PROJ
-VEC_LEN = GAMMA_AT + MODS * PROJ
-
-assert PROJ & (PROJ - 1) == 0
+BETA_AT = GAMMA_AT + MODS * PROJ
+VEC_LEN = BETA_AT + MODS * PROJ
 
 FLOPS = 2 * MODS * P * D * (D + PROJ)
 
@@ -41,11 +41,14 @@ FLOPS = 2 * MODS * P * D * (D + PROJ)
 def load_scale_planes(nc, planes, scales, slot):
     first = slot * PLANES_PER_SLOT
     count = min(PLANES_PER_SLOT, scales.shape[0] - first)
-    for quadrant in range(4):
-        nc.gpsimd.dma_start(
-            out=planes[32 * quadrant : 32 * quadrant + 4 * count, slot, :].bitcast(F32),
-            in_=scales[first : first + count, 4 * quadrant : 4 * quadrant + 4, :].bitcast(F32),
-        )
+    passes_per_dma = count if count == PLANES_PER_SLOT else 1
+    for j in range(0, count, passes_per_dma):
+        for quadrant in range(4):
+            at = 32 * quadrant + 4 * j
+            nc.gpsimd.dma_start(
+                out=planes[at : at + 4 * passes_per_dma, slot, :].bitcast(F32),
+                in_=scales[first + j : first + j + passes_per_dma, 4 * quadrant : 4 * quadrant + 4, :].bitcast(F32),
+            )
 
 
 def weight_scale_plane(planes, g, cols):
@@ -86,14 +89,8 @@ def tile_semanticaligner_w_e_kernel(
         w2_planes = const.tile([P, slots, PROJ], U8, align_bytes=64)
         nc.vector.memset(w2_planes[:].bitcast(I32), 0)
 
-        scale_shift = const.tile([P, MODS, PROJ], BF16)
-        nc.vector.memset(scale_shift[:].rearrange("p m c -> p (m c)").bitcast(I32), 0)
-
         ln_eps = const.tile([P, 1], F32)
         nc.vector.memset(ln_eps[:], LN_EPS)
-        factors = const.tile([P, MODS, P], BF16)
-        nc.vector.memset(factors[:], 0.0)
-
         feats_sb = []
         w1_sb = []
         w2_sb = []
@@ -103,26 +100,27 @@ def tile_semanticaligner_w_e_kernel(
             nc.sync.dma_start(out=f[:], in_=feats[m])
             feats_sb.append(f)
 
-        def load_weight(m, pool, words, n_cols, kept, kind, tapered=False):
-            for g in range(m * PASSES, (m + 1) * PASSES):
-                w = pool.tile([P, PACK * n_cols], U8, name="%s_%d" % (kind, g), tag=kind, align_bytes=64)
-                flat = words[g].rearrange("p n t -> p (n t)")
-                last = g == (m + 1) * PASSES - 1
-                width = N_TILE if tapered and last else n_cols
-                for start in range(0, n_cols, width):
-                    part = slice(PACK * start, PACK * (start + width))
-                    nc.sync.dma_start(out=w[:, part].bitcast(I32), in_=flat[:, part].bitcast(I32))
-                kept.append(w)
+        def load_weight(m, pool, words, n_cols, kept, kind, ranges, pieces):
+            passes = range(m * PASSES, (m + 1) * PASSES)
+            start = 0
+            for width in ranges:
+                for g in passes:
+                    if start == 0:
+                        w = pool.tile([P, PACK * n_cols], U8, name="%s_%d" % (kind, g), tag=kind, align_bytes=64)
+                        kept.append(w)
+                    end = start + width
+                    step = pieces if end == n_cols and g == passes[-1] else width
+                    flat = words[g].rearrange("p n t -> p (n t)")
+                    for at in range(start, end, step):
+                        part = slice(PACK * at, PACK * (at + step))
+                        nc.sync.dma_start(out=kept[g][:, part].bitcast(I32), in_=flat[:, part].bitcast(I32))
+                start += width
 
         def load_vector_rows():
-            for start, vec in ((B1_AT, b1), (B2_AT, b2), (GAMMA_AT, gamma)):
+            for start, vec in ((B1_AT, b1), (B2_AT, b2), (GAMMA_AT, gamma), (BETA_AT, beta)):
                 pieces = vec.rearrange("m (j c) -> (m j) c", c=N_TILE)
                 first_row = start // N_TILE
                 nc.sync.dma_start(out=vec_rows[first_row : first_row + pieces.shape[0], :], in_=pieces)
-
-        def load_scale_shift():
-            for row, vec in ((0, gamma), (1, gamma), (2, beta), (4, beta)):
-                nc.gpsimd.dma_start(out=scale_shift[row : row + 1, :, :], in_=vec.unsqueeze(0))
 
         load_feats(0)
         load_vector_rows()
@@ -136,10 +134,9 @@ def tile_semanticaligner_w_e_kernel(
             (w2_planes, W2_scales, 2),
         ):
             load_scale_planes(nc, planes, scales, slot)
-        load_scale_shift()
         for m in range(MODS):
-            load_weight(m, w1_pool, W1_words, D, w1_sb, "w1")
-            load_weight(m, w2_pool, W2_words, PROJ, w2_sb, "w2", tapered=m == MODS - 1)
+            load_weight(m, w1_pool, W1_words, D, w1_sb, "w1", (D,), D)
+            load_weight(m, w2_pool, W2_words, PROJ, w2_sb, "w2", W2_RANGES[m], N_TILE if m == MODS - 1 else PROJ)
 
         spread = const.tile([P, VEC_LEN], BF16)
 
@@ -194,13 +191,11 @@ def tile_semanticaligner_w_e_kernel(
             codes, planes = operand
             nc.vector.quantize_mx(out=codes[:, g, :].bitcast(FP8X4), scales=planes[:, g, :], in_=grouped[:])
 
-        def make_operand(rows, operand, passes, fill, use=None, after_fill=None):
+        def make_operand(rows, operand, passes, fill, use=None):
             grouped = {}
             for step in range(len(passes) + 3):
                 if step < len(passes):
                     fill(passes[step])
-                    if step == len(passes) - 1 and after_fill:
-                        after_fill()
                 if 1 <= step <= len(passes):
                     g = passes[step - 1]
                     grouped[g] = turn_pass(rows, g)
@@ -237,16 +232,10 @@ def tile_semanticaligner_w_e_kernel(
             nc.scalar.activation(out=unused[:], in_=ln_eps[:], func=func)
 
         tiles = [slice(N_TILE * c, N_TILE * (c + 1)) for c in range(Z_TILES)]
-
-        def new_parts(m):
-            parts = small.tile([P, 2, Z_TILES], F32, name="parts%d" % m, tag="parts")
-            shift = small.tile([P, 1], F32, name="shift%d" % m, tag="shift")
-            return parts, shift
-
         b2_means = const.tile([P, MODS], F32)
-        b2_sums = const.tile([P, MODS], F32)
 
-        def constants_of_norms():
+        def find_b2_means():
+            b2_sums = const.tile([P, MODS], F32)
             for m in range(MODS):
                 unused = scrap.tile([P, N_TILE], BF16, name="unused_s", tag="scalar")
                 nc.scalar.activation(
@@ -254,113 +243,102 @@ def tile_semanticaligner_w_e_kernel(
                     accum_out=b2_sums[:, m : m + 1],
                 )
             nc.vector.tensor_scalar_mul(out=b2_means[:], in0=b2_sums[:], scalar1=1.0 / N_TILE)
-            nc.vector.tensor_scalar_mul(out=scale_shift[0:2, :, :], in0=scale_shift[0:2, :, :], scalar1=-1.0 / PROJ)
 
-        def find_shift(m, bank, shift):
-            unused = scrap.tile([P, N_TILE], BF16, name="unused_s", tag="scalar")
-            total = small.tile([P, 1], F32, name="total", tag="total")
-            nc.scalar.activation(out=unused[:], in_=bank[:], func=ACT.Copy, accum_out=total[:])
-            nc.vector.tensor_scalar(
-                out=shift[:], in0=total[:], scalar1=1.0 / N_TILE, scalar2=b2_means[:, m : m + 1],
-                op0=ALU.mult, op1=ALU.add,
-            )
+        def new_row(name, columns=1):
+            return small.tile([P, columns], F32, name=name, tag=name)
 
-        def shifted(m, c, bank, d, parts, shift):
+        def begin_norm(m):
+            state = {"m": m, "w": z_pool.tile([P, PROJ], F32, name="w", tag="z"), "d": []}
+            state["shift"] = new_row("shift")
+            state["squares"] = new_row("squares", Z_TILES)
+            state["sums"] = new_row("sums", Z_TILES)
+            return state
+
+        def differ(state, bank):
+            m, c = state["m"], len(state["d"])
+            if c == 0:
+                unused = scrap.tile([P, N_TILE], BF16, name="unused_s", tag="scalar")
+                total = new_row("total")
+                nc.scalar.activation(out=unused[:], in_=bank[:], func=ACT.Copy, accum_out=total[:])
+                nc.vector.tensor_scalar(
+                    out=state["shift"][:], in0=total[:], scalar1=1.0 / N_TILE, scalar2=b2_means[:, m : m + 1],
+                    op0=ALU.mult, op1=ALU.add,
+                )
+            d = work.tile([P, N_TILE], F32, name="d", tag="biased")
             nc.vector.scalar_tensor_tensor(
-                out=d, in0=bank[:], scalar=shift[:], in1=spread_vec(B2_AT, m, PROJ, tiles[c]),
-                op0=ALU.subtract, op1=ALU.add, accum_out=parts[:, 1, c : c + 1],
+                out=d[:], in0=bank[:], scalar=state["shift"][:], in1=spread_vec(B2_AT, m, PROJ, tiles[c]),
+                op0=ALU.subtract, op1=ALU.add, accum_out=state["sums"][:, c : c + 1],
             )
-            squares = scrap.tile([P, N_TILE], BF16, name="squares", tag="scalar")
+            unused = scrap.tile([P, N_TILE], BF16, name="unused_q", tag="scalar")
             nc.scalar.activation(
-                out=squares[:], in_=d, func=ACT.Square, scale=PROJ**0.5, accum_out=parts[:, 0, c : c + 1]
+                out=unused[:], in_=d[:], func=ACT.Square, scale=PROJ**-0.5, accum_out=state["squares"][:, c : c + 1]
             )
+            state["d"].append(d)
 
-        def moments(parts):
-            sums = small.tile([P, 3], F32, name="sums", tag="sums")
-            nc.vector.reduce_sum(out=sums[:, 0:2], in_=parts[:], axis=AXIS.X)
-            neg_var = small.tile([P, 1], F32, name="neg_var", tag="neg_var")
+        def finish_norm(state):
+            m, w = state["m"], state["w"]
+            last = Z_TILES - 1
+            sum_most = new_row("sum_most")
+            nc.vector.reduce_sum(out=sum_most[:], in_=state["sums"][:, 0:last], axis=AXIS.X)
+            mu = new_row("mu")
+            nc.vector.tensor_scalar(
+                out=mu[:], in0=state["sums"][:, last : last + 1], scalar1=sum_most[:], scalar2=1.0 / PROJ,
+                op0=ALU.add, op1=ALU.mult,
+            )
+            mu_square = new_row("mu_square")
+            nc.vector.tensor_mul(out=mu_square[:], in0=mu[:], in1=mu[:])
+
+            def centre_and_scale(c):
+                nc.vector.scalar_tensor_tensor(
+                    out=w[:, tiles[c]], in0=state["d"][c][:], scalar=mu[:],
+                    in1=spread_vec(GAMMA_AT, m, PROJ, tiles[c]), op0=ALU.subtract, op1=ALU.mult,
+                )
+
+            centre_and_scale(0)
+            square_most = new_row("square_most")
+            nc.vector.reduce_sum(out=square_most[:], in_=state["squares"][:, 0:last], axis=AXIS.X)
+            centre_and_scale(1)
+            rest = new_row("rest")
             nc.vector.scalar_tensor_tensor(
-                out=neg_var[:], in0=sums[:, 1:2], scalar=sums[:, 1:2], in1=sums[:, 0:1],
-                op0=ALU.mult, op1=ALU.subtract,
+                out=rest[:], in0=square_most[:], scalar=LN_EPS, in1=mu_square[:], op0=ALU.add, op1=ALU.subtract
             )
-            return sums, neg_var
-
-        def gather(m, banks):
-            u = z_pool.tile([P, PROJ], F32, name="u", tag="z")
-            parts, shift = new_parts(m)
-            find_shift(m, banks[0], shift)
-            differences = [work.tile([P, N_TILE], F32, name="d%d" % c, tag="biased") for c in range(Z_TILES)]
-            for c, d in enumerate(differences):
-                shifted(m, c, banks[c], d[:], parts, shift)
-            products = [
-                lambda c=c, d=d: nc.vector.tensor_mul(
-                    out=u[:, tiles[c]], in0=d[:], in1=spread_vec(GAMMA_AT, m, PROJ, tiles[c])
-                )
-                for c, d in enumerate(differences)
-            ]
-            return u, parts, products
-
-        def deviation(m, parts, products):
-            for product in products[0:2]:
-                product()
-            sums, neg_var = moments(parts)
-            total = sums[:, 1:2]
-            std = sums[:, 2:3]
-            for out_std in (std, factors[:, m, 2:3]):
-                nc.scalar.activation(out=out_std, in_=neg_var[:], func=ACT.Sqrt, scale=-1.0 / PROJ**2, bias=ln_eps[:])
-            nc.vector.tensor_copy(out=factors[:, m, 0:1], in_=total)
-            floor = small.tile([P, 1], F32, name="floor", tag="floor")
-            nc.vector.tensor_scalar(
-                out=floor[:], in0=neg_var[:], scalar1=-((NORM_EPS / PROJ) ** 2), scalar2=LN_EPS * NORM_EPS**2,
-                op0=ALU.mult, op1=ALU.add,
+            std = new_row("std")
+            nc.scalar.activation(
+                out=std[:], in_=state["squares"][:, last : last + 1], func=ACT.Sqrt, bias=rest[:]
             )
-            nc.vector.tensor_sub(out=factors[:, m, 1:2], in0=total, in1=factors[:, m, 0:1])
-            nc.vector.tensor_sub(out=factors[:, m, 4:5], in0=std, in1=factors[:, m, 2:3])
-            for product in products[2:]:
-                product()
-            return floor
-
-        def add_row_factors(m, u, floor):
-            factors_psum = turn_pool.tile([P, P], BF16, name="factors_psum", tag="turn")
-            nc.tensor.transpose(factors_psum[:], factors[:, m, :], ident_bf16[:])
-            factors_t = small.tile([P, P], BF16, name="factors_t", tag="factors_t")
-            nc.scalar.copy(out=factors_t[:], in_=factors_psum[:])
-            sumsq = small.tile([P, Z_TILES], F32, name="sumsq", tag="sumsq")
+            for c in range(2, Z_TILES):
+                centre_and_scale(c)
+            shares = new_row("shares", Z_TILES)
             for c in range(Z_TILES):
-                bank = turn_pool.tile([P, N_TILE], F32, name="rows%d" % c, tag="turn")
-                nc.tensor.matmul(
-                    out=bank[:], lhsT=factors_t[:], rhs=scale_shift[:, m, tiles[c]], start=True, stop=True
+                nc.vector.scalar_tensor_tensor(
+                    out=w[:, tiles[c]], in0=spread_vec(BETA_AT, m, PROJ, tiles[c]), scalar=std[:], in1=w[:, tiles[c]],
+                    op0=ALU.mult, op1=ALU.add,
                 )
-                nc.vector.tensor_add(out=u[:, tiles[c]], in0=bank[:], in1=u[:, tiles[c]])
-                squares = scrap.tile([P, N_TILE], BF16, name="squares", tag="scalar")
+                unused = scrap.tile([P, N_TILE], BF16, name="unused_q", tag="scalar")
                 nc.scalar.activation(
-                    out=squares[:], in_=u[:, tiles[c]], func=ACT.Square, accum_out=sumsq[:, c : c + 1]
+                    out=unused[:], in_=w[:, tiles[c]], func=ACT.Square, accum_out=shares[:, c : c + 1]
                 )
-            most = small.tile([P, 1], F32, name="most", tag="most")
-            nc.vector.reduce_sum(out=most[:], in_=sumsq[:, 0 : Z_TILES - 1], axis=AXIS.X)
-            square = small.tile([P, 1], F32, name="square", tag="square")
-            nc.vector.tensor_scalar(
-                out=square[:], in0=sumsq[:, Z_TILES - 1 : Z_TILES], scalar1=most[:], scalar2=floor[:],
-                op0=ALU.add, op1=ALU.max,
-            )
-            return square
-
-        def inverse_norm(square):
-            norm = small.tile([P, 1], F32, name="norm", tag="norm")
-            nc.scalar.sqrt(out=norm[:], in_=square[:])
-            inv_norm = small.tile([P, 1], F32, name="inv_norm", tag="inv_norm")
+            least = new_row("least")
+            nc.vector.tensor_scalar_mul(out=least[:], in0=std[:], scalar1=NORM_EPS)
+            others = new_row("others")
+            nc.vector.reduce_sum(out=others[:], in_=shares[:, 0:last], axis=AXIS.X)
+            norm = new_row("norm")
+            nc.scalar.activation(out=norm[:], in_=shares[:, last : last + 1], func=ACT.Sqrt, bias=others[:])
+            nc.vector.tensor_max(out=norm[:], in0=norm[:], in1=least[:])
+            inv_norm = new_row("inv_norm")
             nc.vector.reciprocal(out=inv_norm[:], in_=norm[:])
             return inv_norm
 
-        def scale_and_store(m, w, inv_norm, which, scalar_tile=None):
-            for c in which:
+        def scale_and_store(state, inv_norm, scalar_tile=None):
+            m, w = state["m"], state["w"]
+            for c in range(Z_TILES):
                 if c == scalar_tile:
                     nc.scalar.activation(out=w[:, tiles[c]], in_=w[:, tiles[c]], func=ACT.Copy, scale=inv_norm[:])
                 else:
                     nc.vector.tensor_scalar_mul(out=w[:, tiles[c]], in0=w[:, tiles[c]], scalar1=inv_norm[:])
                 nc.sync.dma_start(out=out[m][:, tiles[c]], in_=w[:, tiles[c]])
 
-        def two_linears(m, x, after_pass):
+        def two_linears(m, x, after_pass, after_use):
             s_banks = open_banks(H_TILES)
             for i in range(PASSES):
                 mx_pass(m, i, x[0], x[1], w1_sb, w1_planes, 0, s_banks)
@@ -377,13 +355,13 @@ def tile_semanticaligner_w_e_kernel(
 
             def project(i):
                 if i == 0:
-                    z_banks.extend(open_banks(Z_TILES))
+                    z_banks.extend(open_banks(W2_RANGES[m][0] // N_TILE))
                 mx_pass(m, i, operand[0], operand[1], w2_sb, w2_planes, 0, z_banks)
+                after_use()
 
-            make_operand(
-                h, operand, all_passes, bias_and_gelu, use=project, after_fill=lambda: preload_table(ACT.Sqrt)
-            )
-            return z_banks
+            make_operand(h, operand, all_passes, bias_and_gelu, use=project)
+            preload_table(ACT.Sqrt)
+            return operand, z_banks
 
         preload_table(ACT.Gelu)
         pooled = [rows_pool.tile([P, D], BF16, name="pooled%d" % m, tag="rows") for m in range(MODS)]
@@ -405,13 +383,21 @@ def tile_semanticaligner_w_e_kernel(
             elif i < PASSES - 1:
                 spread_next(3)
 
-        z0 = two_linears(0, x[0], between_passes)
-        constants_of_norms()
-        u0, parts0, products0 = gather(0, z0)
-        floor0 = deviation(0, parts0, products0)
-        scale_and_store(0, u0, inverse_norm(add_row_factors(0, u0, floor0)), range(Z_TILES))
+        operand0, z0 = two_linears(0, x[0], between_passes, lambda: spread_next(1))
+        find_b2_means()
+        norm0 = begin_norm(0)
+        for bank in z0:
+            differ(norm0, bank)
+        inv_norm0 = finish_norm(norm0)
         preload_table(ACT.Gelu)
-        z1 = two_linears(1, x[1], lambda i: None)
-        u1, parts1, products1 = gather(1, z1)
-        floor1 = deviation(1, parts1, products1)
-        scale_and_store(1, u1, inverse_norm(add_row_factors(1, u1, floor1)), range(Z_TILES), scalar_tile=1)
+
+        operand1, z1 = two_linears(1, x[1], lambda i: None, lambda: None)
+        scale_and_store(norm0, inv_norm0)
+        norm1 = begin_norm(1)
+        differ(norm1, z1[0])
+        other_banks = open_banks(Z_TILES - 1)
+        for i in range(PASSES):
+            mx_pass(1, i, operand1[0], operand1[1], w2_sb, w2_planes, 1, other_banks)
+        for bank in other_banks:
+            differ(norm1, bank)
+        scale_and_store(norm1, finish_norm(norm1), scalar_tile=1)

from contextlib import ExitStack

import concourse.mybir as mybir
from concourse.masks import make_identity

F32 = mybir.dt.float32
BF16 = mybir.dt.bfloat16
I32 = mybir.dt.int32
U32 = mybir.dt.uint32
U8 = mybir.dt.uint8
FP8X4 = mybir.dt.float8_e4m3fn_x4
ACT = mybir.ActivationFunctionType
ALU = mybir.AluOpType
AXIS = mybir.AxisListType

P = 128
PACK = 4
K_PASS = P * PACK
N_TILE = 512
MODS = 2
STEPS = 2
D = 2560
PROJ = 2048
PASSES = D // K_PASS
H_TILES = D // N_TILE
Z_TILES = PROJ // N_TILE
PLANES_PER_SLOT = 4
W2_RANGES = ((PROJ,), (N_TILE, PROJ - N_TILE))
LN_EPS = 1e-5
NORM_EPS = 1e-12

B1_AT = 0
B2_AT = B1_AT + MODS * D
GAMMA_AT = B2_AT + MODS * PROJ
BETA_AT = GAMMA_AT + MODS * PROJ
VEC_LEN = BETA_AT + MODS * PROJ

FLOPS = 2 * MODS * P * D * (D + PROJ)


def load_scale_planes(nc, planes, scales, slot):
    first = slot * PLANES_PER_SLOT
    count = min(PLANES_PER_SLOT, scales.shape[0] - first)
    passes_per_dma = count if count == PLANES_PER_SLOT else 1
    for j in range(0, count, passes_per_dma):
        for quadrant in range(4):
            at = 32 * quadrant + 4 * j
            nc.gpsimd.dma_start(
                out=planes[at : at + 4 * passes_per_dma, slot, :].bitcast(F32),
                in_=scales[first + j : first + j + passes_per_dma, 4 * quadrant : 4 * quadrant + 4, :].bitcast(F32),
            )


def weight_scale_plane(planes, g, cols):
    return planes[4 * (g % PLANES_PER_SLOT) : P, g // PLANES_PER_SLOT, cols]


def tile_semanticaligner_w_e_kernel(
    tc, feats, W1_words, W1_scales, b1, W2_words, W2_scales, b2, gamma, beta, out
):
    nc = tc.nc
    with ExitStack() as ctx:
        const = ctx.enter_context(tc.tile_pool(name="const", bufs=1))
        w1_pool = ctx.enter_context(tc.tile_pool(name="w1", bufs=6))
        w2_pool = ctx.enter_context(tc.tile_pool(name="w2", bufs=6))
        rows_pool = ctx.enter_context(tc.tile_pool(name="rows", bufs=2))
        operand_pool = ctx.enter_context(tc.tile_pool(name="operand", bufs=2))
        work = ctx.enter_context(tc.tile_pool(name="work", bufs=4))
        scrap = ctx.enter_context(tc.tile_pool(name="scrap", bufs=2))
        z_pool = ctx.enter_context(tc.tile_pool(name="z", bufs=2))
        small = ctx.enter_context(tc.tile_pool(name="small", bufs=2))
        acc_pool = ctx.enter_context(tc.psum_pool(name="acc", bufs=5))
        turn_pool = ctx.enter_context(tc.psum_pool(name="turn", bufs=3))

        ctx.enter_context(tc.manual_schedule())

        ident_f32 = const.tile([P, P], F32)
        make_identity(nc, ident_f32[:])
        ident_bf16 = const.tile([P, P], BF16)
        make_identity(nc, ident_bf16[:])

        vec_rows = const.tile([P, N_TILE], BF16)
        nc.vector.memset(vec_rows[:], 0.0)

        slots = -(-MODS * PASSES // PLANES_PER_SLOT)
        w1_planes = const.tile([P, slots, D], U8, align_bytes=64)
        nc.vector.memset(w1_planes[:].bitcast(I32), 0)

        w2_planes = const.tile([P, slots, PROJ], U8, align_bytes=64)
        nc.vector.memset(w2_planes[:].bitcast(I32), 0)

        ln_eps = const.tile([P, 1], F32)
        nc.vector.memset(ln_eps[:], LN_EPS)
        feats_sb = []
        w1_sb = []
        w2_sb = []

        def load_feats(m):
            f = w1_pool.tile([P, STEPS, D], BF16, name="feats%d" % m, tag="w1", align_bytes=64)
            nc.sync.dma_start(out=f[:], in_=feats[m])
            feats_sb.append(f)

        def load_weight(m, pool, words, n_cols, kept, kind, ranges, pieces):
            passes = range(m * PASSES, (m + 1) * PASSES)
            start = 0
            for width in ranges:
                for g in passes:
                    if start == 0:
                        w = pool.tile([P, PACK * n_cols], U8, name="%s_%d" % (kind, g), tag=kind, align_bytes=64)
                        kept.append(w)
                    end = start + width
                    step = pieces if end == n_cols and g == passes[-1] else width
                    flat = words[g].rearrange("p n t -> p (n t)")
                    for at in range(start, end, step):
                        part = slice(PACK * at, PACK * (at + step))
                        nc.sync.dma_start(out=kept[g][:, part].bitcast(I32), in_=flat[:, part].bitcast(I32))
                start += width

        def load_vector_rows():
            for start, vec in ((B1_AT, b1), (B2_AT, b2), (GAMMA_AT, gamma), (BETA_AT, beta)):
                pieces = vec.rearrange("m (j c) -> (m j) c", c=N_TILE)
                first_row = start // N_TILE
                nc.sync.dma_start(out=vec_rows[first_row : first_row + pieces.shape[0], :], in_=pieces)

        load_feats(0)
        load_vector_rows()
        load_feats(1)
        for planes, scales, slot in (
            (w1_planes, W1_scales, 0),
            (w1_planes, W1_scales, 1),
            (w2_planes, W2_scales, 0),
            (w2_planes, W2_scales, 1),
            (w1_planes, W1_scales, 2),
            (w2_planes, W2_scales, 2),
        ):
            load_scale_planes(nc, planes, scales, slot)
        for m in range(MODS):
            load_weight(m, w1_pool, W1_words, D, w1_sb, "w1", (D,), D)
            load_weight(m, w2_pool, W2_words, PROJ, w2_sb, "w2", W2_RANGES[m], N_TILE if m == MODS - 1 else PROJ)

        spread = const.tile([P, VEC_LEN], BF16)

        def spread_bank(first, on_scalar):
            bank = turn_pool.tile([P, 2 * N_TILE], BF16, name="bank", tag="turn")
            for i in range(2):
                nc.tensor.matmul(
                    out=bank[:, i * N_TILE : (i + 1) * N_TILE],
                    lhsT=ident_bf16[:, first + i : first + i + 1].to_broadcast([P, P]),
                    rhs=vec_rows[:],
                    start=True,
                    stop=True,
                )
            dst = spread[:, first * N_TILE : (first + 2) * N_TILE]
            if on_scalar:
                nc.scalar.copy(out=dst, in_=bank[:])
            else:
                nc.vector.tensor_copy(out=dst, in_=bank[:])

        banks_to_spread = list(range(0, VEC_LEN // N_TILE, 2))

        def spread_next(count):
            for first in banks_to_spread[0:count]:
                spread_bank(first, on_scalar=(first // 2) % 2 == 0)
            del_count = min(count, len(banks_to_spread))
            for unused in range(del_count):
                banks_to_spread.pop(0)

        def spread_vec(start, m, width, cols):
            return spread[:, start + m * width + cols.start : start + m * width + cols.stop]

        def turn_pass(rows, g):
            words = rows[:].bitcast(F32)
            turned = turn_pool.tile([P, 2, P], F32, name="turned", tag="turn")
            for u in range(2):
                nc.tensor.transpose(
                    turned[:, u, :], words[:, (K_PASS // 2) * g + u : (K_PASS // 2) * (g + 1) : 2], ident_f32[:]
                )
            grouped = work.tile([P, P * PACK], BF16, name="grouped", tag="grouped", align_bytes=64)
            nc.scalar.copy(
                out=grouped[:].bitcast(F32).rearrange("p (b u) -> p b u", u=2),
                in_=turned[:].rearrange("p u b -> p b u"),
            )
            return grouped

        def new_operand(kind):
            codes = operand_pool.tile([P, PASSES, P], U32, name=kind + "_codes", tag=kind + "_codes", align_bytes=64)
            planes = operand_pool.tile([P, PASSES, P], U8, name=kind + "_planes", tag=kind + "_planes", align_bytes=64)
            return codes, planes

        def quantise_pass(operand, g, grouped):
            codes, planes = operand
            nc.vector.quantize_mx(out=codes[:, g, :].bitcast(FP8X4), scales=planes[:, g, :], in_=grouped[:])

        def make_operand(rows, operand, passes, fill, use=None):
            grouped = {}
            for step in range(len(passes) + 3):
                if step < len(passes):
                    fill(passes[step])
                if 1 <= step <= len(passes):
                    g = passes[step - 1]
                    grouped[g] = turn_pass(rows, g)
                if 2 <= step <= len(passes) + 1:
                    g = passes[step - 2]
                    quantise_pass(operand, g, grouped[g])
                if step >= 3 and use:
                    use(passes[step - 3])

        def mean_of_steps(m, pooled, g):
            cols = slice(g * K_PASS, (g + 1) * K_PASS)
            total = work.tile([P, K_PASS], BF16, name="total", tag="total")
            nc.vector.tensor_add(out=total[:], in0=feats_sb[m][:, 0, cols], in1=feats_sb[m][:, 1, cols])
            nc.vector.tensor_scalar_mul(out=pooled[:, cols], in0=total[:], scalar1=1.0 / STEPS)

        def open_banks(n_tiles):
            return [acc_pool.tile([P, N_TILE], F32, name="acc%d" % j, tag="acc") for j in range(n_tiles)]

        def mx_pass(m, i, codes, planes, w_sb, w_planes, first_tile, banks):
            g = m * PASSES + i
            for j, bank in enumerate(banks, first_tile):
                nc.tensor.matmul_mx(
                    out=bank[:],
                    lhsT=codes[:, i, :].bitcast(FP8X4),
                    lhsT_scale=planes[:, i, :],
                    rhs=w_sb[g][:, PACK * N_TILE * j : PACK * N_TILE * (j + 1)].bitcast(FP8X4),
                    rhs_scale=weight_scale_plane(w_planes, g, slice(N_TILE * j, N_TILE * (j + 1))),
                    start=(i == 0),
                    stop=(i == PASSES - 1),
                )

        def preload_table(func):
            unused = small.tile([P, 1], F32, name="unused", tag="unused")
            nc.scalar.activation(out=unused[:], in_=ln_eps[:], func=func)

        tiles = [slice(N_TILE * c, N_TILE * (c + 1)) for c in range(Z_TILES)]
        b2_means = const.tile([P, MODS], F32)

        def find_b2_means():
            b2_sums = const.tile([P, MODS], F32)
            for m in range(MODS):
                unused = scrap.tile([P, N_TILE], BF16, name="unused_s", tag="scalar")
                nc.scalar.activation(
                    out=unused[:], in_=spread_vec(B2_AT, m, PROJ, tiles[0]), func=ACT.Copy,
                    accum_out=b2_sums[:, m : m + 1],
                )
            nc.vector.tensor_scalar_mul(out=b2_means[:], in0=b2_sums[:], scalar1=1.0 / N_TILE)

        def new_row(name, columns=1):
            return small.tile([P, columns], F32, name=name, tag=name)

        def begin_norm(m):
            state = {"m": m, "w": z_pool.tile([P, PROJ], F32, name="w", tag="z"), "d": []}
            state["shift"] = new_row("shift")
            state["squares"] = new_row("squares", Z_TILES)
            state["sums"] = new_row("sums", Z_TILES)
            return state

        def differ(state, bank):
            m, c = state["m"], len(state["d"])
            if c == 0:
                unused = scrap.tile([P, N_TILE], BF16, name="unused_s", tag="scalar")
                total = new_row("total")
                nc.scalar.activation(out=unused[:], in_=bank[:], func=ACT.Copy, accum_out=total[:])
                nc.vector.tensor_scalar(
                    out=state["shift"][:], in0=total[:], scalar1=1.0 / N_TILE, scalar2=b2_means[:, m : m + 1],
                    op0=ALU.mult, op1=ALU.add,
                )
            d = work.tile([P, N_TILE], F32, name="d", tag="biased")
            nc.vector.scalar_tensor_tensor(
                out=d[:], in0=bank[:], scalar=state["shift"][:], in1=spread_vec(B2_AT, m, PROJ, tiles[c]),
                op0=ALU.subtract, op1=ALU.add, accum_out=state["sums"][:, c : c + 1],
            )
            unused = scrap.tile([P, N_TILE], BF16, name="unused_q", tag="scalar")
            nc.scalar.activation(
                out=unused[:], in_=d[:], func=ACT.Square, scale=PROJ**-0.5, accum_out=state["squares"][:, c : c + 1]
            )
            state["d"].append(d)

        def finish_norm(state):
            m, w = state["m"], state["w"]
            last = Z_TILES - 1
            sum_most = new_row("sum_most")
            nc.vector.reduce_sum(out=sum_most[:], in_=state["sums"][:, 0:last], axis=AXIS.X)
            mu = new_row("mu")
            nc.vector.tensor_scalar(
                out=mu[:], in0=state["sums"][:, last : last + 1], scalar1=sum_most[:], scalar2=1.0 / PROJ,
                op0=ALU.add, op1=ALU.mult,
            )
            mu_square = new_row("mu_square")
            nc.vector.tensor_mul(out=mu_square[:], in0=mu[:], in1=mu[:])

            def centre_and_scale(c):
                nc.vector.scalar_tensor_tensor(
                    out=w[:, tiles[c]], in0=state["d"][c][:], scalar=mu[:],
                    in1=spread_vec(GAMMA_AT, m, PROJ, tiles[c]), op0=ALU.subtract, op1=ALU.mult,
                )

            centre_and_scale(0)
            square_most = new_row("square_most")
            nc.vector.reduce_sum(out=square_most[:], in_=state["squares"][:, 0:last], axis=AXIS.X)
            centre_and_scale(1)
            rest = new_row("rest")
            nc.vector.scalar_tensor_tensor(
                out=rest[:], in0=square_most[:], scalar=LN_EPS, in1=mu_square[:], op0=ALU.add, op1=ALU.subtract
            )
            std = new_row("std")
            nc.scalar.activation(
                out=std[:], in_=state["squares"][:, last : last + 1], func=ACT.Sqrt, bias=rest[:]
            )
            for c in range(2, Z_TILES):
                centre_and_scale(c)
            shares = new_row("shares", Z_TILES)
            for c in range(Z_TILES):
                nc.vector.scalar_tensor_tensor(
                    out=w[:, tiles[c]], in0=spread_vec(BETA_AT, m, PROJ, tiles[c]), scalar=std[:], in1=w[:, tiles[c]],
                    op0=ALU.mult, op1=ALU.add,
                )
                unused = scrap.tile([P, N_TILE], BF16, name="unused_q", tag="scalar")
                nc.scalar.activation(
                    out=unused[:], in_=w[:, tiles[c]], func=ACT.Square, accum_out=shares[:, c : c + 1]
                )
            least = new_row("least")
            nc.vector.tensor_scalar_mul(out=least[:], in0=std[:], scalar1=NORM_EPS)
            others = new_row("others")
            nc.vector.reduce_sum(out=others[:], in_=shares[:, 0:last], axis=AXIS.X)
            norm = new_row("norm")
            nc.scalar.activation(out=norm[:], in_=shares[:, last : last + 1], func=ACT.Sqrt, bias=others[:])
            nc.vector.tensor_max(out=norm[:], in0=norm[:], in1=least[:])
            inv_norm = new_row("inv_norm")
            nc.vector.reciprocal(out=inv_norm[:], in_=norm[:])
            return inv_norm

        def scale_and_store(state, inv_norm, scalar_tile=None):
            m, w = state["m"], state["w"]
            for c in range(Z_TILES):
                if c == scalar_tile:
                    nc.scalar.activation(out=w[:, tiles[c]], in_=w[:, tiles[c]], func=ACT.Copy, scale=inv_norm[:])
                else:
                    nc.vector.tensor_scalar_mul(out=w[:, tiles[c]], in0=w[:, tiles[c]], scalar1=inv_norm[:])
                nc.sync.dma_start(out=out[m][:, tiles[c]], in_=w[:, tiles[c]])

        def two_linears(m, x, after_pass, after_use):
            s_banks = open_banks(H_TILES)
            for i in range(PASSES):
                mx_pass(m, i, x[0], x[1], w1_sb, w1_planes, 0, s_banks)
                after_pass(i)
            h = rows_pool.tile([P, D], BF16, name="h", tag="rows")
            operand = new_operand("h")
            z_banks = []

            def bias_and_gelu(j):
                biased = work.tile([P, N_TILE], F32, name="biased", tag="biased")
                cols = slice(N_TILE * j, N_TILE * (j + 1))
                nc.vector.tensor_add(out=biased[:], in0=s_banks[j][:], in1=spread_vec(B1_AT, m, D, cols))
                nc.scalar.activation(out=h[:, cols], in_=biased[:], func=ACT.Gelu)

            def project(i):
                if i == 0:
                    z_banks.extend(open_banks(W2_RANGES[m][0] // N_TILE))
                mx_pass(m, i, operand[0], operand[1], w2_sb, w2_planes, 0, z_banks)
                after_use()

            make_operand(h, operand, all_passes, bias_and_gelu, use=project)
            preload_table(ACT.Sqrt)
            return operand, z_banks

        preload_table(ACT.Gelu)
        pooled = [rows_pool.tile([P, D], BF16, name="pooled%d" % m, tag="rows") for m in range(MODS)]
        x = [new_operand("x") for m in range(MODS)]
        all_passes = list(range(PASSES))

        def fill_first(g):
            mean_of_steps(0, pooled[0], g)
            if g > 0:
                spread_next(1)

        make_operand(pooled[0], x[0], all_passes, fill_first)
        for g in all_passes:
            mean_of_steps(1, pooled[1], g)

        def between_passes(i):
            if i == 1:
                make_operand(pooled[1], x[1], all_passes, lambda g: None)
            elif i < PASSES - 1:
                spread_next(3)

        operand0, z0 = two_linears(0, x[0], between_passes, lambda: spread_next(1))
        find_b2_means()
        norm0 = begin_norm(0)
        for bank in z0:
            differ(norm0, bank)
        inv_norm0 = finish_norm(norm0)
        preload_table(ACT.Gelu)

        operand1, z1 = two_linears(1, x[1], lambda i: None, lambda: None)
        scale_and_store(norm0, inv_norm0)
        norm1 = begin_norm(1)
        differ(norm1, z1[0])
        other_banks = open_banks(Z_TILES - 1)
        for i in range(PASSES):
            mx_pass(1, i, operand1[0], operand1[1], w2_sb, w2_planes, 1, other_banks)
        for bank in other_banks:
            differ(norm1, bank)
        scale_and_store(norm1, finish_norm(norm1), scalar_tile=1)
